import numpy as np
import ml_dtypes


def mxq(x, axis, fmt="e4m3"):
    dtype, down = {"e4m3": (ml_dtypes.float8_e4m3fn, 7), "e5m2": (ml_dtypes.float8_e5m2, 14)}[fmt]
    v = np.moveaxis(np.asarray(x, np.float32).astype(ml_dtypes.bfloat16).astype(np.float64), axis, -1)
    blocks = v.reshape(v.shape[:-1] + (-1, 32))
    amax = np.abs(blocks).max(-1, keepdims=True)
    byte = np.maximum(np.where(amax > 0, np.frexp(amax)[1] - 1 + 127, 0) - down, 1)
    scale = np.exp2(byte - 127.0)
    codes = (blocks / scale).astype(np.float32).astype(dtype).astype(np.float64)
    return np.moveaxis((codes * scale).reshape(v.shape), -1, axis)


WIDE = False


def mx_kscale(k):
    if not WIDE:
        return np.ones(k)
    levels = np.array([10, -10, 5, -5, 0])
    a = np.random.permutation(np.resize(levels, k // 512 * 4)).reshape(k // 512, 4)
    idx = np.arange(k)
    return np.exp2(a[idx // 512, idx % 128 // 32])


BF16 = ml_dtypes.bfloat16


def bf(x):
    return np.asarray(x, np.float32).astype(BF16)


def f64(x):
    return np.asarray(x).astype(np.float64)


B, T, D, H, HD, Q_STRIDE, WINDOW, QKV = 1, 1536, 1024, 16, 64, 4, 128, 3
NW = T // (Q_STRIDE * WINDOW)
SEQ = T // NW


def setup_inputs():
    s = mx_kscale(SEQ)
    t = mx_kscale(D)
    g = np.exp(np.random.standard_normal((B, H, NW, SEQ // Q_STRIDE, SEQ)) * 1.3)
    vd = np.random.standard_normal((B, NW, SEQ, D)) * t / s[:, None]
    return {"attn": bf(g / g.sum(-1, keepdims=True) * s),
            "v": bf(np.ascontiguousarray(vd.reshape(B, NW, SEQ, H, HD).transpose(0, 3, 1, 2, 4))),
            "proj_w": bf(np.random.standard_normal((D, D)) * 5.0 / np.sqrt(D) / t[None, :]),
            "proj_b": bf(np.random.standard_normal(D) * 0.2)}


def reference(attn, v, proj_w, proj_b):
    o = mxq(f64(attn), 4, "e4m3") @ mxq(f64(v), 3, "e4m3")
    o = o.transpose(0, 3, 2, 1, 4).reshape(B, -1, H * HD)
    return (mxq(o, 2, "e4m3") @ mxq(f64(proj_w), 1, "e4m3").T) + f64(proj_b)

@@ -1,0 +1,246 @@
+from contextlib import ExitStack
+
+import concourse.mybir as mybir
+from concourse.masks import make_identity
+
+F32 = mybir.dt.float32
+BF16 = mybir.dt.bfloat16
+U32 = mybir.dt.uint32
+U8 = mybir.dt.uint8
+I32 = mybir.dt.int32
+FP8X4 = mybir.dt.float8_e4m3fn_x4
+
+P = 128
+H = 16
+NW = 3
+KEYS = 512
+HD = 64
+D = 1024
+FLOPS = 2 * H * NW * P * KEYS * HD + 2 * NW * P * D * D
+
+PERIOD = 192
+NPAIR = NW * H // 2
+NQUAD = 12
+W_ON_VECTOR = (1, 4, 7, 10, 13)
+
+
+def tile_hieramaskunitattention_pb_kernel(tc, attn, v, proj_w, proj_b, out):
+    nc = tc.nc
+    with ExitStack() as ctx:
+        const = ctx.enter_context(tc.tile_pool(name="const", bufs=1))
+        res = ctx.enter_context(tc.tile_pool(name="res", bufs=1))
+        work = ctx.enter_context(tc.tile_pool(name="work", bufs=2))
+        psum_t = ctx.enter_context(tc.psum_pool(name="psum_t", bufs=4))
+        psum_o = ctx.enter_context(tc.psum_pool(name="psum_o", bufs=2))
+        psum_y = ctx.enter_context(tc.psum_pool(name="psum_y", bufs=2))
+        ctx.enter_context(tc.manual_schedule())
+
+        vq = res.tile([P, (NPAIR + 1) * PERIOD], U32, align_bytes=64)
+        vqs = res.tile([P, (NPAIR + 1) * PERIOD], U8, align_bytes=64)
+        nc.vector.memset(
+            vq[:].bitcast(I32).rearrange("p (a b) -> p a b", b=PERIOD)[:, :, 0:64], 0
+        )
+        nc.vector.memset(
+            vqs[:].bitcast(I32).rearrange("p (a b) -> p a b", b=PERIOD // 4)[:, :, 0:16], 0
+        )
+        brow = const.tile([P, D], BF16)
+        nc.vector.memset(brow[:], 0.0)
+        ones = const.tile([P, P], BF16)
+        nc.vector.memset(ones[:], 1.0)
+        ident_b = const.tile([P, P], BF16)
+        make_identity(nc, ident_b[:])
+        ident_f = const.tile([P, P], F32)
+        make_identity(nc, ident_f[:])
+
+        w_sb = res.tile([P, 8, D], BF16)
+        w_view = proj_w.rearrange("(nt p) k -> p nt k", p=P)
+        nc.sync.dma_start(out=w_sb[:, 0:1, :], in_=w_view[:, 0:1, :])
+        nc.sync.dma_start(out=w_sb[:, 1:2, :], in_=w_view[:, 1:2, :])
+        nc.scalar.dma_start(out=brow[0:1, :], in_=proj_b.rearrange("(o n) -> o n", o=1))
+        for i in range(1, 4):
+            nc.sync.dma_start(out=w_sb[:, 2 * i : 2 * i + 2, :], in_=w_view[:, 2 * i : 2 * i + 2, :])
+        at = {}
+        vraw = {}
+        for s in range(6):
+            w, g = s // 2, s % 2
+            vraw[s] = res.tile([P, 2048], BF16, name="vraw%d" % s)
+            vr = vraw[s][:].rearrange("p (j x f) -> p j x f", x=2, f=256)
+            for x in range(2):
+                h0 = 8 * g + 1 - x
+                nc.sync.dma_start(
+                    out=vr[:, :, x, :],
+                    in_=v[0, h0 : h0 + 7 : 2, w].rearrange("h (p j) c -> p h (j c)", j=4),
+                )
+            for c in (2 * s, 2 * s + 1):
+                at[c] = res.tile([P, 2048], BF16, name="at%d" % c)
+                for hl in range(4):
+                    nc.sync.dma_start(
+                        out=at[c][hl:P:4, :],
+                        in_=attn[0, 4 * (c % 4) + hl, w].rearrange("(a r) k -> a (r k)", r=4),
+                    )
+
+        wg = res.tile([P, 2 * 4096], BF16, align_bytes=64)
+        wq = res.tile([P, 2 * D], U32, align_bytes=64)
+        wqs = res.tile([P, 2 * D], U8, align_bytes=64)
+
+        def wquant(nt):
+            for g in range(2):
+                c0 = D * g + 128 * nt
+                nc.vector.quantize_mx(
+                    out=wq[:, c0 : c0 + 256].bitcast(FP8X4),
+                    scales=wqs[:, c0 : c0 + 256],
+                    in_=wg[:, 4 * c0 : 4 * c0 + 1024],
+                )
+
+        for nt in range(8):
+            for g in range(2):
+                tw = psum_t.tile([P, 4, P], BF16, tag="tp")
+                for t in range(4):
+                    k0 = 512 * g + 128 * t
+                    nc.tensor.transpose(tw[:, t, :], w_sb[:, nt, k0 : k0 + 128], ident_b[:])
+                dst = wg[:, 4096 * g + 512 * nt : 4096 * g + 512 * nt + 512].rearrange("p (n t) -> p n t", t=4)
+                src = tw[:].rearrange("p t n -> p n t")
+                if 2 * nt + g in W_ON_VECTOR:
+                    nc.vector.tensor_copy(out=dst, in_=src)
+                else:
+                    nc.scalar.copy(out=dst, in_=src)
+            if nt % 2 == 1 and nt >= 3:
+                wquant(nt - 3)
+        wquant(6)
+
+        bias_sb = const.tile([P, D], F32)
+        for nh in range(2):
+            pb = psum_y.tile([P, 512], F32, tag="py")
+            nc.tensor.matmul(out=pb[:], lhsT=ones[:], rhs=brow[:, 512 * nh : 512 * nh + 512], start=True, stop=True)
+            nc.scalar.copy(out=bias_sb[:, 512 * nh : 512 * nh + 512], in_=pb[:])
+
+        ag = {}
+        aq = {}
+        aqs = {}
+        po = {}
+        oq = {}
+        oqs = {}
+        py = {}
+        ob = {}
+
+        def vprep(s):
+            vg = work.tile([P, 2048], BF16, tag="vg", align_bytes=64)
+            nc.vector.tensor_copy(
+                out=vg[:, 0:1536].rearrange("p (h c i t) -> p h c t i", h=6, c=16, i=4, t=4),
+                in_=vraw[s][:, 0:1536].rearrange("p (h t c i) -> p h c t i", h=6, t=4, c=16, i=4),
+            )
+            nc.scalar.copy(
+                out=vg[:, 1536:2048].rearrange("p (h c t) -> p h c t", h=2, c=64, t=4),
+                in_=vraw[s][:, 1536:2048].rearrange("p (h t c) -> p h c t", h=2, t=4, c=64),
+            )
+            for j in range(4):
+                c0 = PERIOD * (4 * s + j) + 64
+                nc.vector.quantize_mx(
+                    out=vq[:, c0 : c0 + 128].bitcast(FP8X4),
+                    scales=vqs[:, c0 : c0 + 128],
+                    in_=vg[:, 512 * j : 512 * j + 512],
+                )
+
+        def trans(c):
+            ag[c] = work.tile([P, 2048], BF16, tag="ag", bufs=3, align_bytes=64, name="ag%d" % c)
+            dst = ag[c][:].bitcast(F32).rearrange("p (h a b s) -> p h a b s", h=4, a=32, b=2, s=4)
+            a32 = at[c][:].bitcast(F32)
+            tps = []
+            for b in range(2):
+                tp = psum_t.tile([P, 4, P], F32, tag="tp")
+                tps.append(tp)
+                for rl in range(2):
+                    for u in range(2):
+                        r = 2 * b + rl
+                        nc.tensor.transpose(
+                            tp[:, 2 * rl + u, :], a32[:, 256 * r + u : 256 * r + 256 : 2], ident_f[:]
+                        )
+            for b in range(2):
+                nc.scalar.copy(out=dst[:, :, :, b, :], in_=tps[b][:].rearrange("p s (a h) -> p h a s", h=4))
+
+        def aquant(c):
+            aq[c] = work.tile([P, 512], U32, tag="aq", bufs=3, align_bytes=64, name="aq%d" % c)
+            aqs[c] = work.tile([P, 512], U8, tag="aqs", bufs=3, align_bytes=64, name="aqs%d" % c)
+            nc.vector.quantize_mx(out=aq[c][:].bitcast(FP8X4), scales=aqs[c][:], in_=ag[c][:])
+
+        def stage1(c):
+            s = c // 2
+            if c % 2 == 0:
+                po[s] = psum_o.tile([P, 4, P], F32, tag="po", name="po%d" % s)
+            for jl in range(2):
+                j = 2 * (c % 2) + jl
+                base = PERIOD * (4 * s + j)
+                for hh in range(2):
+                    l0 = base + 128 if hh == 0 else base
+                    r0 = 256 * jl + 128 * hh
+                    nc.tensor.matmul_mx(
+                        out=po[s][:, j, :],
+                        lhsT=vq[:, l0 : l0 + 128].bitcast(FP8X4),
+                        lhsT_scale=vqs[:, l0 : l0 + 128],
+                        rhs=aq[c][:, r0 : r0 + 128].bitcast(FP8X4),
+                        rhs_scale=aqs[c][:, r0 : r0 + 128],
+                        start=(hh == 0),
+                        stop=(hh == 1),
+                    )
+
+        def oprep(s):
+            w, g = s // 2, s % 2
+            og = work.tile([P, 512], BF16, tag="og", align_bytes=64)
+            nc.scalar.copy(out=og[:].rearrange("p (q t) -> p q t", t=4), in_=po[s][:].rearrange("p t q -> p q t"))
+            if g == 0:
+                oq[w] = work.tile([P, 256], U32, tag="oq", align_bytes=64, name="oq%d" % w)
+                oqs[w] = work.tile([P, 256], U8, tag="oqs", align_bytes=64, name="oqs%d" % w)
+            nc.vector.quantize_mx(
+                out=oq[w][:, 128 * g : 128 * g + 128].bitcast(FP8X4),
+                scales=oqs[w][:, 128 * g : 128 * g + 128],
+                in_=og[:],
+            )
+
+        def stage2(w, g):
+            for nh in range(2):
+                if g == 0:
+                    py[(w, nh)] = psum_y.tile([P, 512], F32, tag="py", name="py%d_%d" % (w, nh))
+                c0 = D * g + 512 * nh
+                nc.tensor.matmul_mx(
+                    out=py[(w, nh)][:],
+                    lhsT=oq[w][:, 128 * g : 128 * g + 128].bitcast(FP8X4),
+                    lhsT_scale=oqs[w][:, 128 * g : 128 * g + 128],
+                    rhs=wq[:, c0 : c0 + 512].bitcast(FP8X4),
+                    rhs_scale=wqs[:, c0 : c0 + 512],
+                    start=(g == 0),
+                    stop=(g == 1),
+                )
+
+        out_v = out[0].rearrange("(i w) n -> w i n", w=NW)
+
+        def finish(w, split):
+            ob[w] = work.tile([P, D], F32, tag="ob", name="ob%d" % w)
+            for nh in range(2):
+                cols = slice(512 * nh, 512 * nh + 512)
+                nc.vector.tensor_tensor(
+                    out=ob[w][:, cols], in0=py[(w, nh)][:], in1=bias_sb[:, cols], op=mybir.AluOpType.add
+                )
+                if split:
+                    nc.sync.dma_start(out=out_v[w][:, cols], in_=ob[w][:, cols])
+            if not split:
+                nc.sync.dma_start(out=out_v[w], in_=ob[w][:])
+
+        for c in range(NQUAD):
+            if c % 2 == 0:
+                vprep(c // 2)
+            trans(c)
+            if c >= 1:
+                stage1(c - 1)
+            if c % 4 == 1 and c >= 5:
+                stage2(c // 4 - 1, 0)
+                stage2(c // 4 - 1, 1)
+            aquant(c)
+            if c % 2 == 0 and c >= 2:
+                oprep(c // 2 - 1)
+            if c % 4 == 1 and c >= 5:
+                finish(c // 4 - 1, False)
+        stage2(2, 0)
+        stage1(NQUAD - 1)
+        oprep(5)
+        stage2(2, 1)
+        finish(2, True)

@@ -31,10 +31,31 @@ def tile_hieramaskunitattention_pb_kernel(tc, attn, v, proj_w, proj_b, out):
         res = ctx.enter_context(tc.tile_pool(name="res", bufs=1))
         work = ctx.enter_context(tc.tile_pool(name="work", bufs=2))
         psum_t = ctx.enter_context(tc.psum_pool(name="psum_t", bufs=4))
-        psum_o = ctx.enter_context(tc.psum_pool(name="psum_o", bufs=2))
+        psum_o = ctx.enter_context(tc.psum_pool(name="psum_o", bufs=1))
+        psum_d = ctx.enter_context(tc.psum_pool(name="psum_d", bufs=1))
         psum_y = ctx.enter_context(tc.psum_pool(name="psum_y", bufs=2))
         ctx.enter_context(tc.manual_schedule())
 
+        dz = const.tile([P, 512], U32, align_bytes=64)
+        dzs = const.tile([P, 512], U8, align_bytes=64)
+        zsrc = const.tile([P, 2048], BF16, align_bytes=64)
+        nc.vector.memset(zsrc[:], 0.0)
+        nc.vector.quantize_mx(out=dz[:].bitcast(FP8X4), scales=dzs[:], in_=zsrc[:])
+        pd = psum_d.tile([P, 512], F32)
+
+        def warm(n):
+            for i in range(n):
+                nc.tensor.matmul_mx(
+                    out=pd[:],
+                    lhsT=dz[:, 0:128].bitcast(FP8X4),
+                    lhsT_scale=dzs[:, 0:128],
+                    rhs=dz[:].bitcast(FP8X4),
+                    rhs_scale=dzs[:],
+                    start=True,
+                    stop=True,
+                )
+
+        warm(6)
         vq = res.tile([P, (NPAIR + 1) * PERIOD], U32, align_bytes=64)
         vqs = res.tile([P, (NPAIR + 1) * PERIOD], U8, align_bytes=64)
         nc.vector.memset(
@@ -92,6 +113,7 @@ def tile_hieramaskunitattention_pb_kernel(tc, attn, v, proj_w, proj_b, out):
                     in_=wg[:, 4 * c0 : 4 * c0 + 1024],
                 )
 
+        pb = [psum_y.tile([P, 512], F32, tag="py", name="pb%d" % nh) for nh in range(2)]
         for nt in range(8):
             for g in range(2):
                 tw = psum_t.tile([P, 4, P], BF16, tag="tp")
@@ -104,15 +126,18 @@ def tile_hieramaskunitattention_pb_kernel(tc, attn, v, proj_w, proj_b, out):
                     nc.vector.tensor_copy(out=dst, in_=src)
                 else:
                     nc.scalar.copy(out=dst, in_=src)
+            if nt in (1, 3, 5):
+                for nh in range(2):
+                    nc.tensor.matmul(
+                        out=pb[nh][:], lhsT=ones[:], rhs=brow[:, 512 * nh : 512 * nh + 512], start=True, stop=True
+                    )
             if nt % 2 == 1 and nt >= 3:
                 wquant(nt - 3)
         wquant(6)
-
         bias_sb = const.tile([P, D], F32)
         for nh in range(2):
-            pb = psum_y.tile([P, 512], F32, tag="py")
-            nc.tensor.matmul(out=pb[:], lhsT=ones[:], rhs=brow[:, 512 * nh : 512 * nh + 512], start=True, stop=True)
-            nc.scalar.copy(out=bias_sb[:, 512 * nh : 512 * nh + 512], in_=pb[:])
+            nc.scalar.copy(out=bias_sb[:, 512 * nh : 512 * nh + 512], in_=pb[nh][:])
+        warm(3)
 
         ag = {}
         aq = {}
@@ -196,8 +221,8 @@ def tile_hieramaskunitattention_pb_kernel(tc, attn, v, proj_w, proj_b, out):
                 in_=og[:],
             )
 
-        def stage2(w, g):
-            for nh in range(2):
+        def stage2(w, g, halves):
+            for nh in halves:
                 if g == 0:
                     py[(w, nh)] = psum_y.tile([P, 512], F32, tag="py", name="py%d_%d" % (w, nh))
                 c0 = D * g + 512 * nh
@@ -213,16 +238,16 @@ def tile_hieramaskunitattention_pb_kernel(tc, attn, v, proj_w, proj_b, out):
 
         out_v = out[0].rearrange("(i w) n -> w i n", w=NW)
 
-        def finish(w, split):
-            ob[w] = work.tile([P, D], F32, tag="ob", name="ob%d" % w)
-            for nh in range(2):
-                cols = slice(512 * nh, 512 * nh + 512)
-                nc.vector.tensor_tensor(
-                    out=ob[w][:, cols], in0=py[(w, nh)][:], in1=bias_sb[:, cols], op=mybir.AluOpType.add
-                )
-                if split:
-                    nc.sync.dma_start(out=out_v[w][:, cols], in_=ob[w][:, cols])
-            if not split:
+        def finish(w, nh, split):
+            if nh == 0:
+                ob[w] = work.tile([P, D], F32, tag="ob", name="ob%d" % w)
+            cols = slice(512 * nh, 512 * nh + 512)
+            nc.vector.tensor_tensor(
+                out=ob[w][:, cols], in0=py[(w, nh)][:], in1=bias_sb[:, cols], op=mybir.AluOpType.add
+            )
+            if split:
+                nc.sync.dma_start(out=out_v[w][:, cols], in_=ob[w][:, cols])
+            elif nh == 1:
                 nc.sync.dma_start(out=out_v[w], in_=ob[w][:])
 
         for c in range(NQUAD):
@@ -231,16 +256,21 @@ def tile_hieramaskunitattention_pb_kernel(tc, attn, v, proj_w, proj_b, out):
             trans(c)
             if c >= 1:
                 stage1(c - 1)
-            if c % 4 == 1 and c >= 5:
-                stage2(c // 4 - 1, 0)
-                stage2(c // 4 - 1, 1)
+            nh = c % 4 - 1
+            second = c >= 5 and nh in (0, 1)
+            if second:
+                stage2(c // 4 - 1, 0, (nh,))
+                stage2(c // 4 - 1, 1, (nh,))
+            else:
+                warm(2 if c == 0 else 1)
             aquant(c)
             if c % 2 == 0 and c >= 2:
                 oprep(c // 2 - 1)
-            if c % 4 == 1 and c >= 5:
-                finish(c // 4 - 1, False)
-        stage2(2, 0)
+            if second:
+                finish(c // 4 - 1, nh, False)
+        stage2(2, 0, (0, 1))
         stage1(NQUAD - 1)
         oprep(5)
-        stage2(2, 1)
-        finish(2, True)
+        stage2(2, 1, (0, 1))
+        finish(2, 0, True)
+        finish(2, 1, True)

@@ -21,7 +21,7 @@ FLOPS = 2 * H * NW * P * KEYS * HD + 2 * NW * P * D * D
 PERIOD = 192
 NPAIR = NW * H // 2
 NQUAD = 12
-W_ON_VECTOR = (1, 4, 7, 10, 13)
+W_ON_VECTOR = (2, 6, 10, 14)
 
 
 def tile_hieramaskunitattention_pb_kernel(tc, attn, v, proj_w, proj_b, out):
@@ -31,31 +31,10 @@ def tile_hieramaskunitattention_pb_kernel(tc, attn, v, proj_w, proj_b, out):
         res = ctx.enter_context(tc.tile_pool(name="res", bufs=1))
         work = ctx.enter_context(tc.tile_pool(name="work", bufs=2))
         psum_t = ctx.enter_context(tc.psum_pool(name="psum_t", bufs=4))
-        psum_o = ctx.enter_context(tc.psum_pool(name="psum_o", bufs=1))
-        psum_d = ctx.enter_context(tc.psum_pool(name="psum_d", bufs=1))
+        psum_o = ctx.enter_context(tc.psum_pool(name="psum_o", bufs=2))
         psum_y = ctx.enter_context(tc.psum_pool(name="psum_y", bufs=2))
         ctx.enter_context(tc.manual_schedule())
 
-        dz = const.tile([P, 512], U32, align_bytes=64)
-        dzs = const.tile([P, 512], U8, align_bytes=64)
-        zsrc = const.tile([P, 2048], BF16, align_bytes=64)
-        nc.vector.memset(zsrc[:], 0.0)
-        nc.vector.quantize_mx(out=dz[:].bitcast(FP8X4), scales=dzs[:], in_=zsrc[:])
-        pd = psum_d.tile([P, 512], F32)
-
-        def warm(n):
-            for i in range(n):
-                nc.tensor.matmul_mx(
-                    out=pd[:],
-                    lhsT=dz[:, 0:128].bitcast(FP8X4),
-                    lhsT_scale=dzs[:, 0:128],
-                    rhs=dz[:].bitcast(FP8X4),
-                    rhs_scale=dzs[:],
-                    start=True,
-                    stop=True,
-                )
-
-        warm(6)
         vq = res.tile([P, (NPAIR + 1) * PERIOD], U32, align_bytes=64)
         vqs = res.tile([P, (NPAIR + 1) * PERIOD], U8, align_bytes=64)
         nc.vector.memset(
@@ -72,6 +51,10 @@ def tile_hieramaskunitattention_pb_kernel(tc, attn, v, proj_w, proj_b, out):
         make_identity(nc, ident_b[:])
         ident_f = const.tile([P, P], F32)
         make_identity(nc, ident_f[:])
+        perm = const.tile([P, P], F32)
+        nc.vector.tensor_copy(
+            out=perm[:].rearrange("p (h a) -> p h a", h=2), in_=ident_f[:].rearrange("p (a h) -> p h a", h=2)
+        )
 
         w_sb = res.tile([P, 8, D], BF16)
         w_view = proj_w.rearrange("(nt p) k -> p nt k", p=P)
@@ -93,12 +76,13 @@ def tile_hieramaskunitattention_pb_kernel(tc, attn, v, proj_w, proj_b, out):
                     in_=v[0, h0 : h0 + 7 : 2, w].rearrange("h (p j) c -> p h (j c)", j=4),
                 )
             for c in (2 * s, 2 * s + 1):
-                at[c] = res.tile([P, 2048], BF16, name="at%d" % c)
-                for hl in range(4):
-                    nc.sync.dma_start(
-                        out=at[c][hl:P:4, :],
-                        in_=attn[0, 4 * (c % 4) + hl, w].rearrange("(a r) k -> a (r k)", r=4),
-                    )
+                for jl in range(2):
+                    at[(c, jl)] = res.tile([P, 1024], BF16, name="at%d_%d" % (c, jl))
+                    for hh in range(2):
+                        nc.sync.dma_start(
+                            out=at[(c, jl)][hh:P:2, :],
+                            in_=attn[0, 4 * (c % 4) + 2 * jl + hh, w].rearrange("(a r) k -> a (r k)", r=2),
+                        )
 
         wg = res.tile([P, 2 * 4096], BF16, align_bytes=64)
         wq = res.tile([P, 2 * D], U32, align_bytes=64)
@@ -113,7 +97,6 @@ def tile_hieramaskunitattention_pb_kernel(tc, attn, v, proj_w, proj_b, out):
                     in_=wg[:, 4 * c0 : 4 * c0 + 1024],
                 )
 
-        pb = [psum_y.tile([P, 512], F32, tag="py", name="pb%d" % nh) for nh in range(2)]
         for nt in range(8):
             for g in range(2):
                 tw = psum_t.tile([P, 4, P], BF16, tag="tp")
@@ -126,18 +109,15 @@ def tile_hieramaskunitattention_pb_kernel(tc, attn, v, proj_w, proj_b, out):
                     nc.vector.tensor_copy(out=dst, in_=src)
                 else:
                     nc.scalar.copy(out=dst, in_=src)
-            if nt in (1, 3, 5):
-                for nh in range(2):
-                    nc.tensor.matmul(
-                        out=pb[nh][:], lhsT=ones[:], rhs=brow[:, 512 * nh : 512 * nh + 512], start=True, stop=True
-                    )
             if nt % 2 == 1 and nt >= 3:
                 wquant(nt - 3)
         wquant(6)
+
         bias_sb = const.tile([P, D], F32)
         for nh in range(2):
-            nc.scalar.copy(out=bias_sb[:, 512 * nh : 512 * nh + 512], in_=pb[nh][:])
-        warm(3)
+            pb = psum_y.tile([P, 512], F32, tag="py")
+            nc.tensor.matmul(out=pb[:], lhsT=ones[:], rhs=brow[:, 512 * nh : 512 * nh + 512], start=True, stop=True)
+            nc.scalar.copy(out=bias_sb[:, 512 * nh : 512 * nh + 512], in_=pb[:])
 
         ag = {}
         aq = {}
@@ -151,12 +131,8 @@ def tile_hieramaskunitattention_pb_kernel(tc, attn, v, proj_w, proj_b, out):
         def vprep(s):
             vg = work.tile([P, 2048], BF16, tag="vg", align_bytes=64)
             nc.vector.tensor_copy(
-                out=vg[:, 0:1536].rearrange("p (h c i t) -> p h c t i", h=6, c=16, i=4, t=4),
-                in_=vraw[s][:, 0:1536].rearrange("p (h t c i) -> p h c t i", h=6, t=4, c=16, i=4),
-            )
-            nc.scalar.copy(
-                out=vg[:, 1536:2048].rearrange("p (h c t) -> p h c t", h=2, c=64, t=4),
-                in_=vraw[s][:, 1536:2048].rearrange("p (h t c) -> p h c t", h=2, t=4, c=64),
+                out=vg[:].rearrange("p (h c i t) -> p h c t i", h=8, c=16, i=4, t=4),
+                in_=vraw[s][:].rearrange("p (h t c i) -> p h c t i", h=8, t=4, c=16, i=4),
             )
             for j in range(4):
                 c0 = PERIOD * (4 * s + j) + 64
@@ -168,20 +144,22 @@ def tile_hieramaskunitattention_pb_kernel(tc, attn, v, proj_w, proj_b, out):
 
         def trans(c):
             ag[c] = work.tile([P, 2048], BF16, tag="ag", bufs=3, align_bytes=64, name="ag%d" % c)
-            dst = ag[c][:].bitcast(F32).rearrange("p (h a b s) -> p h a b s", h=4, a=32, b=2, s=4)
-            a32 = at[c][:].bitcast(F32)
+            dst = ag[c][:].bitcast(F32)
             tps = []
-            for b in range(2):
+            for jl in range(2):
+                a32 = at[(c, jl)][:].bitcast(F32)
                 tp = psum_t.tile([P, 4, P], F32, tag="tp")
                 tps.append(tp)
-                for rl in range(2):
+                for r in range(2):
                     for u in range(2):
-                        r = 2 * b + rl
                         nc.tensor.transpose(
-                            tp[:, 2 * rl + u, :], a32[:, 256 * r + u : 256 * r + 256 : 2], ident_f[:]
+                            tp[:, 2 * r + u, :], a32[:, 256 * r + u : 256 * r + 256 : 2], perm[:]
                         )
-            for b in range(2):
-                nc.scalar.copy(out=dst[:, :, :, b, :], in_=tps[b][:].rearrange("p s (a h) -> p h a s", h=4))
+            for jl in range(2):
+                nc.scalar.copy(
+                    out=dst[:, 512 * jl : 512 * jl + 512].rearrange("p (h a s) -> p h a s", h=2, s=4),
+                    in_=tps[jl][:].rearrange("p s (h a) -> p h a s", h=2),
+                )
 
         def aquant(c):
             aq[c] = work.tile([P, 512], U32, tag="aq", bufs=3, align_bytes=64, name="aq%d" % c)
@@ -221,8 +199,8 @@ def tile_hieramaskunitattention_pb_kernel(tc, attn, v, proj_w, proj_b, out):
                 in_=og[:],
             )
 
-        def stage2(w, g, halves):
-            for nh in halves:
+        def stage2(w, g):
+            for nh in range(2):
                 if g == 0:
                     py[(w, nh)] = psum_y.tile([P, 512], F32, tag="py", name="py%d_%d" % (w, nh))
                 c0 = D * g + 512 * nh
@@ -238,16 +216,16 @@ def tile_hieramaskunitattention_pb_kernel(tc, attn, v, proj_w, proj_b, out):
 
         out_v = out[0].rearrange("(i w) n -> w i n", w=NW)
 
-        def finish(w, nh, split):
-            if nh == 0:
-                ob[w] = work.tile([P, D], F32, tag="ob", name="ob%d" % w)
-            cols = slice(512 * nh, 512 * nh + 512)
-            nc.vector.tensor_tensor(
-                out=ob[w][:, cols], in0=py[(w, nh)][:], in1=bias_sb[:, cols], op=mybir.AluOpType.add
-            )
-            if split:
-                nc.sync.dma_start(out=out_v[w][:, cols], in_=ob[w][:, cols])
-            elif nh == 1:
+        def finish(w, split):
+            ob[w] = work.tile([P, D], F32, tag="ob", name="ob%d" % w)
+            for nh in range(2):
+                cols = slice(512 * nh, 512 * nh + 512)
+                nc.vector.tensor_tensor(
+                    out=ob[w][:, cols], in0=py[(w, nh)][:], in1=bias_sb[:, cols], op=mybir.AluOpType.add
+                )
+                if split:
+                    nc.sync.dma_start(out=out_v[w][:, cols], in_=ob[w][:, cols])
+            if not split:
                 nc.sync.dma_start(out=out_v[w], in_=ob[w][:])
 
         for c in range(NQUAD):
@@ -256,21 +234,16 @@ def tile_hieramaskunitattention_pb_kernel(tc, attn, v, proj_w, proj_b, out):
             trans(c)
             if c >= 1:
                 stage1(c - 1)
-            nh = c % 4 - 1
-            second = c >= 5 and nh in (0, 1)
-            if second:
-                stage2(c // 4 - 1, 0, (nh,))
-                stage2(c // 4 - 1, 1, (nh,))
-            else:
-                warm(2 if c == 0 else 1)
+            if c % 4 == 1 and c >= 5:
+                stage2(c // 4 - 1, 0)
+                stage2(c // 4 - 1, 1)
             aquant(c)
             if c % 2 == 0 and c >= 2:
                 oprep(c // 2 - 1)
-            if second:
-                finish(c // 4 - 1, nh, False)
-        stage2(2, 0, (0, 1))
+            if c % 4 == 1 and c >= 5:
+                finish(c // 4 - 1, False)
+        stage2(2, 0)
         stage1(NQUAD - 1)
         oprep(5)
-        stage2(2, 1, (0, 1))
-        finish(2, 0, True)
-        finish(2, 1, True)
+        stage2(2, 1)
+        finish(2, True)

@@ -67,22 +67,24 @@ def tile_hieramaskunitattention_pb_kernel(tc, attn, v, proj_w, proj_b, out):
         vraw = {}
         for s in range(6):
             w, g = s // 2, s % 2
-            vraw[s] = res.tile([P, 2048], BF16, name="vraw%d" % s)
-            vr = vraw[s][:].rearrange("p (j x f) -> p j x f", x=2, f=256)
-            for x in range(2):
-                h0 = 8 * g + 1 - x
-                nc.sync.dma_start(
-                    out=vr[:, :, x, :],
-                    in_=v[0, h0 : h0 + 7 : 2, w].rearrange("h (p j) c -> p h (j c)", j=4),
-                )
-            for c in (2 * s, 2 * s + 1):
-                for jl in range(2):
-                    at[(c, jl)] = res.tile([P, 1024], BF16, name="at%d_%d" % (c, jl))
-                    for hh in range(2):
-                        nc.sync.dma_start(
-                            out=at[(c, jl)][hh:P:2, :],
-                            in_=attn[0, 4 * (c % 4) + 2 * jl + hh, w].rearrange("(a r) k -> a (r k)", r=2),
-                        )
+            if g == 0:
+                vraw[w] = res.tile([P, 4096], BF16, name="vraw%d" % w)
+                vr = vraw[w][:].rearrange("p (j x f) -> p j x f", x=2, f=256)
+                for x in range(2):
+                    nc.sync.dma_start(
+                        out=vr[:, :, x, :],
+                        in_=v[0, 1 - x : H : 2, w].rearrange("h (p j) c -> p h (j c)", j=4),
+                    )
+            at[s] = res.tile([P, 4096], BF16, name="at%d" % s)
+            pieces = 2 if s == 5 else 1
+            n = 4 // pieces
+            for i in range(pieces):
+                for hh in range(2):
+                    h0 = 8 * g + 2 * n * i + hh
+                    nc.sync.dma_start(
+                        out=at[s][hh:P:2, 1024 * n * i : 1024 * n * (i + 1)].rearrange("a (j f) -> a j f", j=n),
+                        in_=attn[0, h0 : h0 + 2 * n - 1 : 2, w].rearrange("h (a r) k -> a h (r k)", r=2),
+                    )
 
         wg = res.tile([P, 2 * 4096], BF16, align_bytes=64)
         wq = res.tile([P, 2 * D], U32, align_bytes=64)
@@ -132,7 +134,9 @@ def tile_hieramaskunitattention_pb_kernel(tc, attn, v, proj_w, proj_b, out):
             vg = work.tile([P, 2048], BF16, tag="vg", align_bytes=64)
             nc.vector.tensor_copy(
                 out=vg[:].rearrange("p (h c i t) -> p h c t i", h=8, c=16, i=4, t=4),
-                in_=vraw[s][:].rearrange("p (h t c i) -> p h c t i", h=8, t=4, c=16, i=4),
+                in_=vraw[s // 2][:, 2048 * (s % 2) : 2048 * (s % 2) + 2048].rearrange(
+                    "p (h t c i) -> p h c t i", h=8, t=4, c=16, i=4
+                ),
             )
             for j in range(4):
                 c0 = PERIOD * (4 * s + j) + 64
@@ -147,7 +151,8 @@ def tile_hieramaskunitattention_pb_kernel(tc, attn, v, proj_w, proj_b, out):
             dst = ag[c][:].bitcast(F32)
             tps = []
             for jl in range(2):
-                a32 = at[(c, jl)][:].bitcast(F32)
+                j = 2 * (c % 2) + jl
+                a32 = at[c // 2][:, 1024 * j : 1024 * j + 1024].bitcast(F32)
                 tp = psum_t.tile([P, 4, P], F32, tag="tp")
                 tps.append(tp)
                 for r in range(2):

@@ -22,6 +22,9 @@ PERIOD = 192
 NPAIR = NW * H // 2
 NQUAD = 12
 W_ON_VECTOR = (2, 6, 10, 14)
+ORDER = "AAAAAA"
+DUMMY_N = 512
+ACT_HEADS = 2
 
 
 def tile_hieramaskunitattention_pb_kernel(tc, attn, v, proj_w, proj_b, out):
@@ -31,10 +34,35 @@ def tile_hieramaskunitattention_pb_kernel(tc, attn, v, proj_w, proj_b, out):
         res = ctx.enter_context(tc.tile_pool(name="res", bufs=1))
         work = ctx.enter_context(tc.tile_pool(name="work", bufs=2))
         psum_t = ctx.enter_context(tc.psum_pool(name="psum_t", bufs=4))
-        psum_o = ctx.enter_context(tc.psum_pool(name="psum_o", bufs=2))
+        psum_o = ctx.enter_context(tc.psum_pool(name="psum_o", bufs=1))
+        psum_d = ctx.enter_context(tc.psum_pool(name="psum_d", bufs=1))
         psum_y = ctx.enter_context(tc.psum_pool(name="psum_y", bufs=2))
         ctx.enter_context(tc.manual_schedule())
 
+        dz = const.tile([P, 512], U32, align_bytes=64)
+        dzs = const.tile([P, 512], U8, align_bytes=64)
+        zsrc = const.tile([P, 2048], BF16, align_bytes=64)
+        nc.vector.memset(zsrc[:].bitcast(I32), 0)
+        nc.vector.quantize_mx(out=dz[:].bitcast(FP8X4), scales=dzs[:], in_=zsrc[:])
+        pd = psum_d.tile([P, 512], F32)
+
+        def warm(n, width):
+            for i in range(n):
+                nc.tensor.matmul_mx(
+                    out=pd[:, 0:width],
+                    lhsT=dz[:, 0:128].bitcast(FP8X4),
+                    lhsT_scale=dzs[:, 0:128],
+                    rhs=dz[:, 0:width].bitcast(FP8X4),
+                    rhs_scale=dzs[:, 0:width],
+                    start=True,
+                    stop=True,
+                )
+
+        warm(3, 512)
+        brow = const.tile([P, D], BF16)
+        nc.vector.memset(brow[:].bitcast(I32), 0)
+        ones = const.tile([P, P], BF16)
+        nc.vector.memset(ones[:], 1.0)
         vq = res.tile([P, (NPAIR + 1) * PERIOD], U32, align_bytes=64)
         vqs = res.tile([P, (NPAIR + 1) * PERIOD], U8, align_bytes=64)
         nc.vector.memset(
@@ -43,10 +71,6 @@ def tile_hieramaskunitattention_pb_kernel(tc, attn, v, proj_w, proj_b, out):
         nc.vector.memset(
             vqs[:].bitcast(I32).rearrange("p (a b) -> p a b", b=PERIOD // 4)[:, :, 0:16], 0
         )
-        brow = const.tile([P, D], BF16)
-        nc.vector.memset(brow[:], 0.0)
-        ones = const.tile([P, P], BF16)
-        nc.vector.memset(ones[:], 1.0)
         ident_b = const.tile([P, P], BF16)
         make_identity(nc, ident_b[:])
         ident_f = const.tile([P, P], F32)
@@ -67,24 +91,27 @@ def tile_hieramaskunitattention_pb_kernel(tc, attn, v, proj_w, proj_b, out):
         vraw = {}
         for s in range(6):
             w, g = s // 2, s % 2
-            if g == 0:
-                vraw[w] = res.tile([P, 4096], BF16, name="vraw%d" % w)
-                vr = vraw[w][:].rearrange("p (j x f) -> p j x f", x=2, f=256)
-                for x in range(2):
-                    nc.sync.dma_start(
-                        out=vr[:, :, x, :],
-                        in_=v[0, 1 - x : H : 2, w].rearrange("h (p j) c -> p h (j c)", j=4),
-                    )
-            at[s] = res.tile([P, 4096], BF16, name="at%d" % s)
-            pieces = 2 if s == 5 else 1
-            n = 4 // pieces
-            for i in range(pieces):
-                for hh in range(2):
-                    h0 = 8 * g + 2 * n * i + hh
-                    nc.sync.dma_start(
-                        out=at[s][hh:P:2, 1024 * n * i : 1024 * n * (i + 1)].rearrange("a (j f) -> a j f", j=n),
-                        in_=attn[0, h0 : h0 + 2 * n - 1 : 2, w].rearrange("h (a r) k -> a h (r k)", r=2),
-                    )
+            vraw[s] = res.tile([P, 2048], BF16, name="vraw%d" % s)
+            vr = vraw[s][:].rearrange("p (j x f) -> p j x f", x=2, f=256)
+            for x in range(2):
+                h0 = 8 * g + 1 - x
+                heads = v[0, h0 : h0 + 7 : 2, w]
+                if ORDER[s] == "B":
+                    nc.sync.dma_start(out=vr[:, :, x, :], in_=heads.rearrange("h (p j) c -> p h (j c)", j=4))
+                else:
+                    for u in range(2):
+                        nc.sync.dma_start(
+                            out=vr[:, :, x, 128 * u : 128 * u + 128],
+                            in_=heads[:, 256 * u : 256 * u + 256, :].rearrange("h (p e) c -> p h (e c)", e=2),
+                        )
+            for c in (2 * s, 2 * s + 1):
+                for jl in range(2):
+                    at[(c, jl)] = res.tile([P, 1024], BF16, name="at%d_%d" % (c, jl))
+                    for hh in range(2):
+                        nc.sync.dma_start(
+                            out=at[(c, jl)][hh:P:2, :],
+                            in_=attn[0, 4 * (c % 4) + 2 * jl + hh, w].rearrange("(a r) k -> a (r k)", r=2),
+                        )
 
         wg = res.tile([P, 2 * 4096], BF16, align_bytes=64)
         wq = res.tile([P, 2 * D], U32, align_bytes=64)
@@ -99,6 +126,7 @@ def tile_hieramaskunitattention_pb_kernel(tc, attn, v, proj_w, proj_b, out):
                     in_=wg[:, 4 * c0 : 4 * c0 + 1024],
                 )
 
+        pb = [psum_y.tile([P, 512], F32, tag="py", name="pb%d" % nh) for nh in range(2)]
         for nt in range(8):
             for g in range(2):
                 tw = psum_t.tile([P, 4, P], BF16, tag="tp")
@@ -111,15 +139,18 @@ def tile_hieramaskunitattention_pb_kernel(tc, attn, v, proj_w, proj_b, out):
                     nc.vector.tensor_copy(out=dst, in_=src)
                 else:
                     nc.scalar.copy(out=dst, in_=src)
+            if nt in (1, 3, 5):
+                for nh in range(2):
+                    nc.tensor.matmul(
+                        out=pb[nh][:], lhsT=ones[:], rhs=brow[:, 512 * nh : 512 * nh + 512], start=True, stop=True
+                    )
             if nt % 2 == 1 and nt >= 3:
                 wquant(nt - 3)
         wquant(6)
-
         bias_sb = const.tile([P, D], F32)
         for nh in range(2):
-            pb = psum_y.tile([P, 512], F32, tag="py")
-            nc.tensor.matmul(out=pb[:], lhsT=ones[:], rhs=brow[:, 512 * nh : 512 * nh + 512], start=True, stop=True)
-            nc.scalar.copy(out=bias_sb[:, 512 * nh : 512 * nh + 512], in_=pb[:])
+            nc.scalar.copy(out=bias_sb[:, 512 * nh : 512 * nh + 512], in_=pb[nh][:])
+        warm(4, 512)
 
         ag = {}
         aq = {}
@@ -132,12 +163,16 @@ def tile_hieramaskunitattention_pb_kernel(tc, attn, v, proj_w, proj_b, out):
 
         def vprep(s):
             vg = work.tile([P, 2048], BF16, tag="vg", align_bytes=64)
+            nv = 256 * (8 - ACT_HEADS)
             nc.vector.tensor_copy(
-                out=vg[:].rearrange("p (h c i t) -> p h c t i", h=8, c=16, i=4, t=4),
-                in_=vraw[s // 2][:, 2048 * (s % 2) : 2048 * (s % 2) + 2048].rearrange(
-                    "p (h t c i) -> p h c t i", h=8, t=4, c=16, i=4
-                ),
+                out=vg[:, 0:nv].rearrange("p (h c i t) -> p h c t i", c=16, i=4, t=4),
+                in_=vraw[s][:, 0:nv].rearrange("p (h t c i) -> p h c t i", t=4, c=16, i=4),
             )
+            if ACT_HEADS:
+                nc.scalar.copy(
+                    out=vg[:, nv:2048].rearrange("p (h c t) -> p h c t", c=64, t=4),
+                    in_=vraw[s][:, nv:2048].rearrange("p (h t c) -> p h c t", t=4, c=64),
+                )
             for j in range(4):
                 c0 = PERIOD * (4 * s + j) + 64
                 nc.vector.quantize_mx(
@@ -146,30 +181,39 @@ def tile_hieramaskunitattention_pb_kernel(tc, attn, v, proj_w, proj_b, out):
                     in_=vg[:, 512 * j : 512 * j + 512],
                 )
 
-        def trans(c):
+        def trans(c, split):
             ag[c] = work.tile([P, 2048], BF16, tag="ag", bufs=3, align_bytes=64, name="ag%d" % c)
             dst = ag[c][:].bitcast(F32)
             tps = []
             for jl in range(2):
-                j = 2 * (c % 2) + jl
-                a32 = at[c // 2][:, 1024 * j : 1024 * j + 1024].bitcast(F32)
+                a32 = at[(c, jl)][:].bitcast(F32)
                 tp = psum_t.tile([P, 4, P], F32, tag="tp")
                 tps.append(tp)
                 for r in range(2):
                     for u in range(2):
-                        nc.tensor.transpose(
-                            tp[:, 2 * r + u, :], a32[:, 256 * r + u : 256 * r + 256 : 2], perm[:]
-                        )
+                        if ORDER[c // 2] == "B":
+                            words = a32[:, 256 * r + u : 256 * r + 256 : 2]
+                        else:
+                            words = a32[:, 256 * r + 128 * u : 256 * r + 128 * u + 128]
+                        nc.tensor.transpose(tp[:, 2 * r + u, :], words, perm[:])
             for jl in range(2):
-                nc.scalar.copy(
-                    out=dst[:, 512 * jl : 512 * jl + 512].rearrange("p (h a s) -> p h a s", h=2, s=4),
-                    in_=tps[jl][:].rearrange("p s (h a) -> p h a s", h=2),
-                )
+                o_ap = dst[:, 512 * jl : 512 * jl + 512].rearrange("p (h a s) -> p h a s", h=2, s=4)
+                i_ap = tps[jl][:].rearrange("p s (h a) -> p h a s", h=2)
+                if split and jl == 1:
+                    nc.vector.tensor_copy(out=o_ap, in_=i_ap)
+                else:
+                    nc.scalar.copy(out=o_ap, in_=i_ap)
 
-        def aquant(c):
+        def aquant(c, pieces):
             aq[c] = work.tile([P, 512], U32, tag="aq", bufs=3, align_bytes=64, name="aq%d" % c)
             aqs[c] = work.tile([P, 512], U8, tag="aqs", bufs=3, align_bytes=64, name="aqs%d" % c)
-            nc.vector.quantize_mx(out=aq[c][:].bitcast(FP8X4), scales=aqs[c][:], in_=ag[c][:])
+            n = 512 // pieces
+            for i in range(pieces):
+                nc.vector.quantize_mx(
+                    out=aq[c][:, n * i : n * i + n].bitcast(FP8X4),
+                    scales=aqs[c][:, n * i : n * i + n],
+                    in_=ag[c][:, 4 * n * i : 4 * n * i + 4 * n],
+                )
 
         def stage1(c):
             s = c // 2
@@ -204,51 +248,58 @@ def tile_hieramaskunitattention_pb_kernel(tc, attn, v, proj_w, proj_b, out):
                 in_=og[:],
             )
 
-        def stage2(w, g):
-            for nh in range(2):
-                if g == 0:
-                    py[(w, nh)] = psum_y.tile([P, 512], F32, tag="py", name="py%d_%d" % (w, nh))
-                c0 = D * g + 512 * nh
-                nc.tensor.matmul_mx(
-                    out=py[(w, nh)][:],
-                    lhsT=oq[w][:, 128 * g : 128 * g + 128].bitcast(FP8X4),
-                    lhsT_scale=oqs[w][:, 128 * g : 128 * g + 128],
-                    rhs=wq[:, c0 : c0 + 512].bitcast(FP8X4),
-                    rhs_scale=wqs[:, c0 : c0 + 512],
-                    start=(g == 0),
-                    stop=(g == 1),
-                )
+        def stage2(s, nh):
+            w, g = s // 2, s % 2
+            if g == 0:
+                py[(w, nh)] = psum_y.tile([P, 512], F32, tag="py", name="py%d_%d" % (w, nh))
+            c0 = D * g + 512 * nh
+            nc.tensor.matmul_mx(
+                out=py[(w, nh)][:],
+                lhsT=oq[w][:, 128 * g : 128 * g + 128].bitcast(FP8X4),
+                lhsT_scale=oqs[w][:, 128 * g : 128 * g + 128],
+                rhs=wq[:, c0 : c0 + 512].bitcast(FP8X4),
+                rhs_scale=wqs[:, c0 : c0 + 512],
+                start=(g == 0),
+                stop=(g == 1),
+            )
 
         out_v = out[0].rearrange("(i w) n -> w i n", w=NW)
 
-        def finish(w, split):
-            ob[w] = work.tile([P, D], F32, tag="ob", name="ob%d" % w)
-            for nh in range(2):
-                cols = slice(512 * nh, 512 * nh + 512)
-                nc.vector.tensor_tensor(
-                    out=ob[w][:, cols], in0=py[(w, nh)][:], in1=bias_sb[:, cols], op=mybir.AluOpType.add
-                )
-                if split:
-                    nc.sync.dma_start(out=out_v[w][:, cols], in_=ob[w][:, cols])
-            if not split:
+        def finish(w, nh, split):
+            if nh == 0:
+                ob[w] = work.tile([P, D], F32, tag="ob", name="ob%d" % w)
+            cols = slice(512 * nh, 512 * nh + 512)
+            nc.vector.tensor_tensor(
+                out=ob[w][:, cols], in0=py[(w, nh)][:], in1=bias_sb[:, cols], op=mybir.AluOpType.add
+            )
+            if split:
+                nc.sync.dma_start(out=out_v[w][:, cols], in_=ob[w][:, cols])
+            elif nh == 1:
                 nc.sync.dma_start(out=out_v[w], in_=ob[w][:])
 
         for c in range(NQUAD):
+            last = c == NQUAD - 1
             if c % 2 == 0:
                 vprep(c // 2)
-            trans(c)
+            trans(c, last)
             if c >= 1:
                 stage1(c - 1)
-            if c % 4 == 1 and c >= 5:
-                stage2(c // 4 - 1, 0)
-                stage2(c // 4 - 1, 1)
-            aquant(c)
+            if c >= 3:
+                s2, nh = (c - 3) // 2, (c - 3) % 2
+                stage2(s2, nh)
+                if DUMMY_N:
+                    warm(1, DUMMY_N)
+            else:
+                warm(2, 512)
+            aquant(c, 2 if last else 1)
             if c % 2 == 0 and c >= 2:
                 oprep(c // 2 - 1)
-            if c % 4 == 1 and c >= 5:
-                finish(c // 4 - 1, False)
-        stage2(2, 0)
+            if c >= 3 and s2 % 2 == 1:
+                finish(s2 // 2, nh, False)
+        stage2(4, 1)
         stage1(NQUAD - 1)
         oprep(5)
-        stage2(2, 1)
-        finish(2, True)
+        stage2(5, 0)
+        stage2(5, 1)
+        finish(2, 0, True)
+        finish(2, 1, True)

@@ -22,9 +22,9 @@ PERIOD = 192
 NPAIR = NW * H // 2
 NQUAD = 12
 W_ON_VECTOR = (2, 6, 10, 14)
-ORDER = "AAAAAA"
-DUMMY_N = 512
-ACT_HEADS = 2
+ORDER = "BBBBBB"
+S1_LAG = 3
+ACT_HEADS = 0
 
 
 def tile_hieramaskunitattention_pb_kernel(tc, attn, v, proj_w, proj_b, out):
@@ -34,31 +34,10 @@ def tile_hieramaskunitattention_pb_kernel(tc, attn, v, proj_w, proj_b, out):
         res = ctx.enter_context(tc.tile_pool(name="res", bufs=1))
         work = ctx.enter_context(tc.tile_pool(name="work", bufs=2))
         psum_t = ctx.enter_context(tc.psum_pool(name="psum_t", bufs=4))
-        psum_o = ctx.enter_context(tc.psum_pool(name="psum_o", bufs=1))
-        psum_d = ctx.enter_context(tc.psum_pool(name="psum_d", bufs=1))
+        psum_o = ctx.enter_context(tc.psum_pool(name="psum_o", bufs=2))
         psum_y = ctx.enter_context(tc.psum_pool(name="psum_y", bufs=2))
         ctx.enter_context(tc.manual_schedule())
 
-        dz = const.tile([P, 512], U32, align_bytes=64)
-        dzs = const.tile([P, 512], U8, align_bytes=64)
-        zsrc = const.tile([P, 2048], BF16, align_bytes=64)
-        nc.vector.memset(zsrc[:].bitcast(I32), 0)
-        nc.vector.quantize_mx(out=dz[:].bitcast(FP8X4), scales=dzs[:], in_=zsrc[:])
-        pd = psum_d.tile([P, 512], F32)
-
-        def warm(n, width):
-            for i in range(n):
-                nc.tensor.matmul_mx(
-                    out=pd[:, 0:width],
-                    lhsT=dz[:, 0:128].bitcast(FP8X4),
-                    lhsT_scale=dzs[:, 0:128],
-                    rhs=dz[:, 0:width].bitcast(FP8X4),
-                    rhs_scale=dzs[:, 0:width],
-                    start=True,
-                    stop=True,
-                )
-
-        warm(3, 512)
         brow = const.tile([P, D], BF16)
         nc.vector.memset(brow[:].bitcast(I32), 0)
         ones = const.tile([P, P], BF16)
@@ -139,23 +118,21 @@ def tile_hieramaskunitattention_pb_kernel(tc, attn, v, proj_w, proj_b, out):
                     nc.vector.tensor_copy(out=dst, in_=src)
                 else:
                     nc.scalar.copy(out=dst, in_=src)
-            if nt in (1, 3, 5):
-                for nh in range(2):
-                    nc.tensor.matmul(
-                        out=pb[nh][:], lhsT=ones[:], rhs=brow[:, 512 * nh : 512 * nh + 512], start=True, stop=True
-                    )
             if nt % 2 == 1 and nt >= 3:
                 wquant(nt - 3)
         wquant(6)
         bias_sb = const.tile([P, D], F32)
         for nh in range(2):
+            nc.tensor.matmul(
+                out=pb[nh][:], lhsT=ones[:], rhs=brow[:, 512 * nh : 512 * nh + 512], start=True, stop=True
+            )
             nc.scalar.copy(out=bias_sb[:, 512 * nh : 512 * nh + 512], in_=pb[nh][:])
-        warm(4, 512)
 
         ag = {}
         aq = {}
         aqs = {}
         po = {}
+        og = {}
         oq = {}
         oqs = {}
         py = {}
@@ -205,8 +182,8 @@ def tile_hieramaskunitattention_pb_kernel(tc, attn, v, proj_w, proj_b, out):
                     nc.scalar.copy(out=o_ap, in_=i_ap)
 
         def aquant(c, pieces):
-            aq[c] = work.tile([P, 512], U32, tag="aq", bufs=3, align_bytes=64, name="aq%d" % c)
-            aqs[c] = work.tile([P, 512], U8, tag="aqs", bufs=3, align_bytes=64, name="aqs%d" % c)
+            aq[c] = work.tile([P, 512], U32, tag="aq", bufs=5, align_bytes=64, name="aq%d" % c)
+            aqs[c] = work.tile([P, 512], U8, tag="aqs", bufs=5, align_bytes=64, name="aqs%d" % c)
             n = 512 // pieces
             for i in range(pieces):
                 nc.vector.quantize_mx(
@@ -235,17 +212,19 @@ def tile_hieramaskunitattention_pb_kernel(tc, attn, v, proj_w, proj_b, out):
                         stop=(hh == 1),
                     )
 
-        def oprep(s):
+        def ocopy(s):
+            og[s] = work.tile([P, 512], BF16, tag="og", align_bytes=64, name="og%d" % s)
+            nc.scalar.copy(out=og[s][:].rearrange("p (q t) -> p q t", t=4), in_=po[s][:].rearrange("p t q -> p q t"))
+
+        def oquant(s):
             w, g = s // 2, s % 2
-            og = work.tile([P, 512], BF16, tag="og", align_bytes=64)
-            nc.scalar.copy(out=og[:].rearrange("p (q t) -> p q t", t=4), in_=po[s][:].rearrange("p t q -> p q t"))
             if g == 0:
                 oq[w] = work.tile([P, 256], U32, tag="oq", align_bytes=64, name="oq%d" % w)
                 oqs[w] = work.tile([P, 256], U8, tag="oqs", align_bytes=64, name="oqs%d" % w)
             nc.vector.quantize_mx(
                 out=oq[w][:, 128 * g : 128 * g + 128].bitcast(FP8X4),
                 scales=oqs[w][:, 128 * g : 128 * g + 128],
-                in_=og[:],
+                in_=og[s][:],
             )
 
         def stage2(s, nh):
@@ -277,29 +256,27 @@ def tile_hieramaskunitattention_pb_kernel(tc, attn, v, proj_w, proj_b, out):
             elif nh == 1:
                 nc.sync.dma_start(out=out_v[w], in_=ob[w][:])
 
-        for c in range(NQUAD):
-            last = c == NQUAD - 1
-            if c % 2 == 0:
-                vprep(c // 2)
-            trans(c, last)
-            if c >= 1:
-                stage1(c - 1)
-            if c >= 3:
-                s2, nh = (c - 3) // 2, (c - 3) % 2
-                stage2(s2, nh)
-                if DUMMY_N:
-                    warm(1, DUMMY_N)
-            else:
-                warm(2, 512)
-            aquant(c, 2 if last else 1)
-            if c % 2 == 0 and c >= 2:
-                oprep(c // 2 - 1)
-            if c >= 3 and s2 % 2 == 1:
-                finish(s2 // 2, nh, False)
-        stage2(4, 1)
-        stage1(NQUAD - 1)
-        oprep(5)
-        stage2(5, 0)
-        stage2(5, 1)
-        finish(2, 0, True)
-        finish(2, 1, True)
+        for st in range(2 * 5 + 6 + 2):
+            for s in range(6):
+                if st == max(0, 2 * s - 1):
+                    vprep(s)
+            if st < NQUAD:
+                trans(st, st == NQUAD - 1)
+            if 0 <= st - S1_LAG < NQUAD:
+                stage1(st - S1_LAG)
+            done = []
+            for s in range(6):
+                for nh in range(2):
+                    if st == 2 * s + 6 + nh:
+                        stage2(s, nh)
+                        if s % 2 == 1:
+                            done.append((s // 2, nh))
+            ready = [s for s in range(6) if st == 2 * s + 4]
+            for s in ready:
+                ocopy(s)
+            for w, nh in done:
+                finish(w, nh, w == NW - 1)
+            if st < NQUAD:
+                aquant(st, 2 if st == NQUAD - 1 else 1)
+            for s in ready:
+                oquant(s)

@@ -21,10 +21,13 @@ FLOPS = 2 * H * NW * P * KEYS * HD + 2 * NW * P * D * D
 PERIOD = 192
 NPAIR = NW * H // 2
 NQUAD = 12
-W_ON_VECTOR = (2, 6, 10, 14)
+NGROUP = 6
+
+LOADS = "w0 w1 v0 w2 w3 v1 w4 w5 w6 w7 a0 a1 a2 v2 a3 a4 v3 a5 a6 v4 a7 a8 v5 a9 a10 a11"
+PLAN = "w0 w1 w2 c0 w3 w4 q0 c1 w5 W0 W1 q1 w6 w7 W2 W3 b0 b1 a0 A0 c2 a1 A1 q2 a2 A2 c3 a3 s0 A3 q3 a4 s1 o0 A4 O0 c4 a5 s2 A5 q4 a6 s3 y0 o1 A6 O1 c5 a7 s4 y1 A7 q5 a8 s5 y2 o2 f0 A8 O2 a9 s6 y3 f1 A9 a10 s7 y4 o3 A10 O3 a11 s8 y5 B11 s9 y6 o4 f2 O4 s10 y7 f3 s11 y8 o5 O5 y9 y10 f4 y11 f5"
 ORDER = "BBBBBB"
-S1_LAG = 3
 ACT_HEADS = 0
+V_LAST = ()
 
 
 def tile_hieramaskunitattention_pb_kernel(tc, attn, v, proj_w, proj_b, out):
@@ -38,10 +41,18 @@ def tile_hieramaskunitattention_pb_kernel(tc, attn, v, proj_w, proj_b, out):
         psum_y = ctx.enter_context(tc.psum_pool(name="psum_y", bufs=2))
         ctx.enter_context(tc.manual_schedule())
 
-        brow = const.tile([P, D], BF16)
-        nc.vector.memset(brow[:].bitcast(I32), 0)
         ones = const.tile([P, P], BF16)
         nc.vector.memset(ones[:], 1.0)
+        ident_b = const.tile([P, P], BF16)
+        make_identity(nc, ident_b[:])
+        ident_f = const.tile([P, P], F32)
+        make_identity(nc, ident_f[:])
+        brow = const.tile([P, D], BF16)
+        nc.vector.memset(brow[:].bitcast(I32), 0)
+        perm = const.tile([P, P], F32)
+        nc.vector.tensor_copy(
+            out=perm[:].rearrange("p (h a) -> p h a", h=2), in_=ident_f[:].rearrange("p (a h) -> p h a", h=2)
+        )
         vq = res.tile([P, (NPAIR + 1) * PERIOD], U32, align_bytes=64)
         vqs = res.tile([P, (NPAIR + 1) * PERIOD], U8, align_bytes=64)
         nc.vector.memset(
@@ -50,25 +61,16 @@ def tile_hieramaskunitattention_pb_kernel(tc, attn, v, proj_w, proj_b, out):
         nc.vector.memset(
             vqs[:].bitcast(I32).rearrange("p (a b) -> p a b", b=PERIOD // 4)[:, :, 0:16], 0
         )
-        ident_b = const.tile([P, P], BF16)
-        make_identity(nc, ident_b[:])
-        ident_f = const.tile([P, P], F32)
-        make_identity(nc, ident_f[:])
-        perm = const.tile([P, P], F32)
-        nc.vector.tensor_copy(
-            out=perm[:].rearrange("p (h a) -> p h a", h=2), in_=ident_f[:].rearrange("p (a h) -> p h a", h=2)
-        )
 
-        w_sb = res.tile([P, 8, D], BF16)
-        w_view = proj_w.rearrange("(nt p) k -> p nt k", p=P)
-        nc.sync.dma_start(out=w_sb[:, 0:1, :], in_=w_view[:, 0:1, :])
-        nc.sync.dma_start(out=w_sb[:, 1:2, :], in_=w_view[:, 1:2, :])
-        nc.scalar.dma_start(out=brow[0:1, :], in_=proj_b.rearrange("(o n) -> o n", o=1))
-        for i in range(1, 4):
-            nc.sync.dma_start(out=w_sb[:, 2 * i : 2 * i + 2, :], in_=w_view[:, 2 * i : 2 * i + 2, :])
+        w_sb = {}
         at = {}
         vraw = {}
-        for s in range(6):
+
+        def load_w(nt):
+            w_sb[nt] = res.tile([P, D], BF16, name="w%d" % nt)
+            nc.sync.dma_start(out=w_sb[nt][:], in_=proj_w[128 * nt : 128 * nt + 128, :])
+
+        def load_v(s):
             w, g = s // 2, s % 2
             vraw[s] = res.tile([P, 2048], BF16, name="vraw%d" % s)
             vr = vraw[s][:].rearrange("p (j x f) -> p j x f", x=2, f=256)
@@ -83,51 +85,57 @@ def tile_hieramaskunitattention_pb_kernel(tc, attn, v, proj_w, proj_b, out):
                             out=vr[:, :, x, 128 * u : 128 * u + 128],
                             in_=heads[:, 256 * u : 256 * u + 256, :].rearrange("h (p e) c -> p h (e c)", e=2),
                         )
-            for c in (2 * s, 2 * s + 1):
-                for jl in range(2):
-                    at[(c, jl)] = res.tile([P, 1024], BF16, name="at%d_%d" % (c, jl))
-                    for hh in range(2):
-                        nc.sync.dma_start(
-                            out=at[(c, jl)][hh:P:2, :],
-                            in_=attn[0, 4 * (c % 4) + 2 * jl + hh, w].rearrange("(a r) k -> a (r k)", r=2),
-                        )
+
+        def load_a(c):
+            for jl in range(2):
+                at[(c, jl)] = res.tile([P, 1024], BF16, name="at%d_%d" % (c, jl))
+                for hh in range(2):
+                    nc.sync.dma_start(
+                        out=at[(c, jl)][hh:P:2, :],
+                        in_=attn[0, 4 * (c % 4) + 2 * jl + hh, c // 4].rearrange("(a r) k -> a (r k)", r=2),
+                    )
+
+        nc.scalar.dma_start(out=brow[0:1, :], in_=proj_b.rearrange("(o n) -> o n", o=1))
+        for item in LOADS.split(" "):
+            what, i = item[0:1], int(item[1:])
+            if what == "w":
+                load_w(i)
+            elif what == "v":
+                load_v(i)
+            else:
+                load_a(i)
 
         wg = res.tile([P, 2 * 4096], BF16, align_bytes=64)
         wq = res.tile([P, 2 * D], U32, align_bytes=64)
         wqs = res.tile([P, 2 * D], U8, align_bytes=64)
 
-        def wquant(nt):
-            for g in range(2):
-                c0 = D * g + 128 * nt
+        def wtrans(nt):
+            tw = psum_t.tile([P, 8, P], BF16, tag="tp")
+            for k in range(8):
+                nc.tensor.transpose(tw[:, k, :], w_sb[nt][:, 128 * k : 128 * k + 128], ident_b[:])
+            dst = wg[:].rearrange("p (g n t) -> p g n t", g=2, t=4)[:, :, 128 * nt : 128 * nt + 128, :]
+            nc.scalar.copy(out=dst, in_=tw[:].rearrange("p (g t) n -> p g n t", g=2))
+
+        def wquant(nh, g):
+            if True:
+                c0 = D * g + 512 * nh
                 nc.vector.quantize_mx(
-                    out=wq[:, c0 : c0 + 256].bitcast(FP8X4),
-                    scales=wqs[:, c0 : c0 + 256],
-                    in_=wg[:, 4 * c0 : 4 * c0 + 1024],
+                    out=wq[:, c0 : c0 + 512].bitcast(FP8X4),
+                    scales=wqs[:, c0 : c0 + 512],
+                    in_=wg[:, 4 * c0 : 4 * c0 + 2048],
                 )
 
-        pb = [psum_y.tile([P, 512], F32, tag="py", name="pb%d" % nh) for nh in range(2)]
-        for nt in range(8):
-            for g in range(2):
-                tw = psum_t.tile([P, 4, P], BF16, tag="tp")
-                for t in range(4):
-                    k0 = 512 * g + 128 * t
-                    nc.tensor.transpose(tw[:, t, :], w_sb[:, nt, k0 : k0 + 128], ident_b[:])
-                dst = wg[:, 4096 * g + 512 * nt : 4096 * g + 512 * nt + 512].rearrange("p (n t) -> p n t", t=4)
-                src = tw[:].rearrange("p t n -> p n t")
-                if 2 * nt + g in W_ON_VECTOR:
-                    nc.vector.tensor_copy(out=dst, in_=src)
-                else:
-                    nc.scalar.copy(out=dst, in_=src)
-            if nt % 2 == 1 and nt >= 3:
-                wquant(nt - 3)
-        wquant(6)
         bias_sb = const.tile([P, D], F32)
-        for nh in range(2):
-            nc.tensor.matmul(
-                out=pb[nh][:], lhsT=ones[:], rhs=brow[:, 512 * nh : 512 * nh + 512], start=True, stop=True
-            )
-            nc.scalar.copy(out=bias_sb[:, 512 * nh : 512 * nh + 512], in_=pb[nh][:])
 
+        pbs = [psum_y.tile([P, 512], F32, tag="py", name="pb%d" % nh) for nh in range(2)]
+
+        def bias(nh):
+            if True:
+                pb = pbs[nh]
+                nc.tensor.matmul(out=pb[:], lhsT=ones[:], rhs=brow[:, 512 * nh : 512 * nh + 512], start=True, stop=True)
+                nc.scalar.copy(out=bias_sb[:, 512 * nh : 512 * nh + 512], in_=pb[:])
+
+        vg = {}
         ag = {}
         aq = {}
         aqs = {}
@@ -138,65 +146,67 @@ def tile_hieramaskunitattention_pb_kernel(tc, attn, v, proj_w, proj_b, out):
         py = {}
         ob = {}
 
-        def vprep(s):
-            vg = work.tile([P, 2048], BF16, tag="vg", align_bytes=64)
+        def vcopy(s):
+            vg[s] = work.tile([P, 2048], BF16, tag="vg", align_bytes=64, name="vg%d" % s)
             nv = 256 * (8 - ACT_HEADS)
             nc.vector.tensor_copy(
-                out=vg[:, 0:nv].rearrange("p (h c i t) -> p h c t i", c=16, i=4, t=4),
+                out=vg[s][:, 0:nv].rearrange("p (h c i t) -> p h c t i", c=16, i=4, t=4),
                 in_=vraw[s][:, 0:nv].rearrange("p (h t c i) -> p h c t i", t=4, c=16, i=4),
             )
             if ACT_HEADS:
                 nc.scalar.copy(
-                    out=vg[:, nv:2048].rearrange("p (h c t) -> p h c t", c=64, t=4),
-                    in_=vraw[s][:, nv:2048].rearrange("p (h t c) -> p h c t", t=4, c=64),
+                    out=vg[s][:, nv:2048].rearrange("p (h c i t) -> p h c t i", c=16, i=4, t=4),
+                    in_=vraw[s][:, nv:2048].rearrange("p (h t c i) -> p h c t i", t=4, c=16, i=4),
                 )
+
+        def vquant(s):
             for j in range(4):
                 c0 = PERIOD * (4 * s + j) + 64
                 nc.vector.quantize_mx(
                     out=vq[:, c0 : c0 + 128].bitcast(FP8X4),
                     scales=vqs[:, c0 : c0 + 128],
-                    in_=vg[:, 512 * j : 512 * j + 512],
+                    in_=vg[s][:, 512 * j : 512 * j + 512],
                 )
 
-        def trans(c, split):
-            ag[c] = work.tile([P, 2048], BF16, tag="ag", bufs=3, align_bytes=64, name="ag%d" % c)
+        def trans(c, banks):
+            if 0 in banks:
+                ag[c] = work.tile([P, 2048], BF16, tag="ag", bufs=3, align_bytes=64, name="ag%d" % c)
             dst = ag[c][:].bitcast(F32)
-            tps = []
-            for jl in range(2):
-                a32 = at[(c, jl)][:].bitcast(F32)
+            for b in banks:
+                a32 = at[(c, b)][:].bitcast(F32)
                 tp = psum_t.tile([P, 4, P], F32, tag="tp")
-                tps.append(tp)
                 for r in range(2):
                     for u in range(2):
+                        k0 = 256 * r
                         if ORDER[c // 2] == "B":
-                            words = a32[:, 256 * r + u : 256 * r + 256 : 2]
+                            words = a32[:, k0 + u : k0 + 256 : 2]
                         else:
-                            words = a32[:, 256 * r + 128 * u : 256 * r + 128 * u + 128]
+                            words = a32[:, k0 + 128 * u : k0 + 128 * u + 128]
                         nc.tensor.transpose(tp[:, 2 * r + u, :], words, perm[:])
-            for jl in range(2):
-                o_ap = dst[:, 512 * jl : 512 * jl + 512].rearrange("p (h a s) -> p h a s", h=2, s=4)
-                i_ap = tps[jl][:].rearrange("p s (h a) -> p h a s", h=2)
-                if split and jl == 1:
+                o_ap = dst[:, 512 * b : 512 * b + 512].rearrange("p (i s) -> p i s", s=4)
+                i_ap = tp[:].rearrange("p s i -> p i s")
+                if 2 * c + b in V_LAST:
                     nc.vector.tensor_copy(out=o_ap, in_=i_ap)
                 else:
                     nc.scalar.copy(out=o_ap, in_=i_ap)
 
-        def aquant(c, pieces):
-            aq[c] = work.tile([P, 512], U32, tag="aq", bufs=5, align_bytes=64, name="aq%d" % c)
-            aqs[c] = work.tile([P, 512], U8, tag="aqs", bufs=5, align_bytes=64, name="aqs%d" % c)
+        def aquant(c, pieces, which):
+            if 0 in which:
+                aq[c] = work.tile([P, 512], U32, tag="aq", bufs=5, align_bytes=64, name="aq%d" % c)
+                aqs[c] = work.tile([P, 512], U8, tag="aqs", bufs=5, align_bytes=64, name="aqs%d" % c)
             n = 512 // pieces
-            for i in range(pieces):
+            for i in which:
                 nc.vector.quantize_mx(
                     out=aq[c][:, n * i : n * i + n].bitcast(FP8X4),
                     scales=aqs[c][:, n * i : n * i + n],
                     in_=ag[c][:, 4 * n * i : 4 * n * i + 4 * n],
                 )
 
-        def stage1(c):
+        def stage1(c, pairs):
             s = c // 2
-            if c % 2 == 0:
+            if c % 2 == 0 and 0 in pairs:
                 po[s] = psum_o.tile([P, 4, P], F32, tag="po", name="po%d" % s)
-            for jl in range(2):
+            for jl in pairs:
                 j = 2 * (c % 2) + jl
                 base = PERIOD * (4 * s + j)
                 for hh in range(2):
@@ -244,39 +254,45 @@ def tile_hieramaskunitattention_pb_kernel(tc, attn, v, proj_w, proj_b, out):
 
         out_v = out[0].rearrange("(i w) n -> w i n", w=NW)
 
-        def finish(w, nh, split):
-            if nh == 0:
-                ob[w] = work.tile([P, D], F32, tag="ob", name="ob%d" % w)
+        def finish(w, nh):
+            ob[(w, nh)] = work.tile([P, 512], F32, tag="ob", bufs=4, name="ob%d_%d" % (w, nh))
             cols = slice(512 * nh, 512 * nh + 512)
             nc.vector.tensor_tensor(
-                out=ob[w][:, cols], in0=py[(w, nh)][:], in1=bias_sb[:, cols], op=mybir.AluOpType.add
+                out=ob[(w, nh)][:], in0=py[(w, nh)][:], in1=bias_sb[:, cols], op=mybir.AluOpType.add
             )
-            if split:
-                nc.sync.dma_start(out=out_v[w][:, cols], in_=ob[w][:, cols])
-            elif nh == 1:
-                nc.sync.dma_start(out=out_v[w], in_=ob[w][:])
+            nc.sync.dma_start(out=out_v[w][:, cols], in_=ob[(w, nh)][:])
 
-        for st in range(2 * 5 + 6 + 2):
-            for s in range(6):
-                if st == max(0, 2 * s - 1):
-                    vprep(s)
-            if st < NQUAD:
-                trans(st, st == NQUAD - 1)
-            if 0 <= st - S1_LAG < NQUAD:
-                stage1(st - S1_LAG)
-            done = []
-            for s in range(6):
-                for nh in range(2):
-                    if st == 2 * s + 6 + nh:
-                        stage2(s, nh)
-                        if s % 2 == 1:
-                            done.append((s // 2, nh))
-            ready = [s for s in range(6) if st == 2 * s + 4]
-            for s in ready:
-                ocopy(s)
-            for w, nh in done:
-                finish(w, nh, w == NW - 1)
-            if st < NQUAD:
-                aquant(st, 2 if st == NQUAD - 1 else 1)
-            for s in ready:
-                oquant(s)
+        for item in PLAN.split(" "):
+            what, i = item[0:1], int(item[1:]) if len(item) > 1 else 0
+            if what == "b":
+                bias(i)
+            elif what == "w":
+                wtrans(i)
+            elif what == "W":
+                wquant(i // 2, i % 2)
+            elif what == "c":
+                vcopy(i)
+            elif what == "q":
+                vquant(i)
+            elif what == "a":
+                trans(i, (0, 1))
+            elif what == "x":
+                trans(i // 2, (i % 2,))
+            elif what == "H":
+                aquant(i // 2, 2, (i % 2,))
+            elif what == "S":
+                stage1(i // 2, (i % 2,))
+            elif what == "A":
+                aquant(i, 1, (0,))
+            elif what == "B":
+                aquant(i, 2, (0, 1))
+            elif what == "s":
+                stage1(i, (0, 1))
+            elif what == "o":
+                ocopy(i)
+            elif what == "O":
+                oquant(i)
+            elif what == "y":
+                stage2(i // 2, i % 2)
+            elif what == "f":
+                finish(i // 2, i % 2)

@@ -87,13 +87,13 @@ def tile_hieramaskunitattention_pb_kernel(tc, attn, v, proj_w, proj_b, out):
                         )
 
         def load_a(c):
-            for jl in range(2):
-                at[(c, jl)] = res.tile([P, 1024], BF16, name="at%d_%d" % (c, jl))
-                for hh in range(2):
-                    nc.sync.dma_start(
-                        out=at[(c, jl)][hh:P:2, :],
-                        in_=attn[0, 4 * (c % 4) + 2 * jl + hh, c // 4].rearrange("(a r) k -> a (r k)", r=2),
-                    )
+            at[c] = res.tile([P, 2, 1024], BF16, name="at%d" % c)
+            h0 = 4 * (c % 4)
+            for hh in range(2):
+                nc.sync.dma_start(
+                    out=at[c][hh:P:2, :, :],
+                    in_=attn[0, h0 + hh : h0 + hh + 3 : 2, c // 4].rearrange("h (a r) k -> a h (r k)", r=2),
+                )
 
         nc.scalar.dma_start(out=brow[0:1, :], in_=proj_b.rearrange("(o n) -> o n", o=1))
         for item in LOADS.split(" "):
@@ -173,7 +173,7 @@ def tile_hieramaskunitattention_pb_kernel(tc, attn, v, proj_w, proj_b, out):
                 ag[c] = work.tile([P, 2048], BF16, tag="ag", bufs=3, align_bytes=64, name="ag%d" % c)
             dst = ag[c][:].bitcast(F32)
             for b in banks:
-                a32 = at[(c, b)][:].bitcast(F32)
+                a32 = at[c][:, b, :].bitcast(F32)
                 tp = psum_t.tile([P, 4, P], F32, tag="tp")
                 for r in range(2):
                     for u in range(2):

@@ -23,8 +23,8 @@ NPAIR = NW * H // 2
 NQUAD = 12
 NGROUP = 6
 
-LOADS = "w0 w1 v0 w2 w3 v1 w4 w5 w6 w7 a0 a1 a2 v2 a3 a4 v3 a5 a6 v4 a7 a8 v5 a9 a10 a11"
-PLAN = "w0 w1 w2 c0 w3 w4 q0 c1 w5 W0 W1 q1 w6 w7 W2 W3 b0 b1 a0 A0 c2 a1 A1 q2 a2 A2 c3 a3 s0 A3 q3 a4 s1 o0 A4 O0 c4 a5 s2 A5 q4 a6 s3 y0 o1 A6 O1 c5 a7 s4 y1 A7 q5 a8 s5 y2 o2 f0 A8 O2 a9 s6 y3 f1 A9 a10 s7 y4 o3 A10 O3 a11 s8 y5 B11 s9 y6 o4 f2 O4 s10 y7 f3 s11 y8 o5 O5 y9 y10 f4 y11 f5"
+LOADS = "w0 w1 v0 w2 w3 w4 w5 w6 w7 a0 a1 v1 a2 a3 v2 a4 a5 v3 a6 a7 v4 a8 a9 v5 a10 a11"
+PLAN = "w0 w1 w2 c0 w3 q0 w4 w5 w6 W0 W1 w7 W2 W3 a0 A0 c1 a1 A1 q1 b0 b1 a2 s0 A2 c2 a3 s1 o0 A3 q2 O0 a4 s2 A4 c3 a5 s3 y0 o1 A5 q3 O1 a6 s4 y1 A6 c4 a7 s5 y2 o2 A7 f0 q4 O2 a8 s6 y3 A8 f1 c5 a9 s7 y4 o3 A9 q5 O3 a10 s8 y5 A10 a11 s9 y6 o4 B11 f2 O4 s10 y7 f3 s11 y8 o5 O5 y9 y10 f4 y11 f5"
 ORDER = "BBBBBB"
 ACT_HEADS = 0
 V_LAST = ()
@@ -170,7 +170,7 @@ def tile_hieramaskunitattention_pb_kernel(tc, attn, v, proj_w, proj_b, out):
 
         def trans(c, banks):
             if 0 in banks:
-                ag[c] = work.tile([P, 2048], BF16, tag="ag", bufs=3, align_bytes=64, name="ag%d" % c)
+                ag[c] = work.tile([P, 2048], BF16, tag="ag", bufs=4, align_bytes=64, name="ag%d" % c)
             dst = ag[c][:].bitcast(F32)
             for b in banks:
                 a32 = at[c][:, b, :].bitcast(F32)
@@ -192,8 +192,8 @@ def tile_hieramaskunitattention_pb_kernel(tc, attn, v, proj_w, proj_b, out):
 
         def aquant(c, pieces, which):
             if 0 in which:
-                aq[c] = work.tile([P, 512], U32, tag="aq", bufs=5, align_bytes=64, name="aq%d" % c)
-                aqs[c] = work.tile([P, 512], U8, tag="aqs", bufs=5, align_bytes=64, name="aqs%d" % c)
+                aq[c] = work.tile([P, 512], U32, tag="aq", bufs=6, align_bytes=64, name="aq%d" % c)
+                aqs[c] = work.tile([P, 512], U8, tag="aqs", bufs=6, align_bytes=64, name="aqs%d" % c)
             n = 512 // pieces
             for i in which:
                 nc.vector.quantize_mx(

@@ -23,8 +23,8 @@ NPAIR = NW * H // 2
 NQUAD = 12
 NGROUP = 6
 
-LOADS = "w0 w1 v0 w2 w3 w4 w5 w6 w7 a0 a1 v1 a2 a3 v2 a4 a5 v3 a6 a7 v4 a8 a9 v5 a10 a11"
-PLAN = "w0 w1 w2 c0 w3 q0 w4 w5 w6 W0 W1 w7 W2 W3 a0 A0 c1 a1 A1 q1 b0 b1 a2 s0 A2 c2 a3 s1 o0 A3 q2 O0 a4 s2 A4 c3 a5 s3 y0 o1 A5 q3 O1 a6 s4 y1 A6 c4 a7 s5 y2 o2 A7 f0 q4 O2 a8 s6 y3 A8 f1 c5 a9 s7 y4 o3 A9 q5 O3 a10 s8 y5 A10 a11 s9 y6 o4 B11 f2 O4 s10 y7 f3 s11 y8 o5 O5 y9 y10 f4 y11 f5"
+LOADS = "w0 w1 x1 v0 x2 x3 a0 a1 v1 a2 a3 v2 a4 a5 v3 a6 a7 v4 a8 a9 v5 a10 a11"
+PLAN = "w0 w1 w2 c0 w3 q0 w4 w5 w6 W0 W1 w7 W2 W3 a0 A0 c1 a1 A1 q1 b0 b1 a2 s0 A2 c2 a3 s1 o0 A3 q2 O0 a4 s2 A4 c3 a5 s3 y0 o1 A5 q3 O1 a6 s4 y1 A6 c4 a7 s5 y2 o2 A7 f0 q4 O2 a8 s6 y3 A8 f1 c5 a9 s7 y4 o3 A9 q5 O3 a10 s8 y5 A10 a11 s9 y6 o4 B11 f2 O4 s10 y7 f3 s11 o5 O5 z0 Z0 F0 z1 Z1 F1 z2 Z2 F2 z3 Z3 F3"
 ORDER = "BBBBBB"
 ACT_HEADS = 0
 V_LAST = ()
@@ -66,9 +66,12 @@ def tile_hieramaskunitattention_pb_kernel(tc, attn, v, proj_w, proj_b, out):
         at = {}
         vraw = {}
 
-        def load_w(nt):
-            w_sb[nt] = res.tile([P, D], BF16, name="w%d" % nt)
-            nc.sync.dma_start(out=w_sb[nt][:], in_=proj_w[128 * nt : 128 * nt + 128, :])
+        def load_w(nt, n):
+            t = res.tile([P, n, D], BF16, name="w%d" % nt)
+            rows = proj_w[128 * nt : 128 * nt + 128 * n, :]
+            nc.sync.dma_start(out=t[:], in_=rows.rearrange("(n p) k -> p n k", p=P))
+            for i in range(n):
+                w_sb[nt + i] = t[:, i, :]
 
         def load_v(s):
             w, g = s // 2, s % 2
@@ -99,7 +102,9 @@ def tile_hieramaskunitattention_pb_kernel(tc, attn, v, proj_w, proj_b, out):
         for item in LOADS.split(" "):
             what, i = item[0:1], int(item[1:])
             if what == "w":
-                load_w(i)
+                load_w(i, 1)
+            elif what == "x":
+                load_w(2 * i, 2)
             elif what == "v":
                 load_v(i)
             else:
@@ -252,7 +257,31 @@ def tile_hieramaskunitattention_pb_kernel(tc, attn, v, proj_w, proj_b, out):
                 stop=(g == 1),
             )
 
+        def piece(q, g):
+            w = NW - 1
+            if g == 0:
+                py[(w, 4 + q)] = psum_t.tile([P, 256], F32, tag="tp", name="pz%d" % q)
+            c0 = D * g + 256 * q
+            nc.tensor.matmul_mx(
+                out=py[(w, 4 + q)][:],
+                lhsT=oq[w][:, 128 * g : 128 * g + 128].bitcast(FP8X4),
+                lhsT_scale=oqs[w][:, 128 * g : 128 * g + 128],
+                rhs=wq[:, c0 : c0 + 256].bitcast(FP8X4),
+                rhs_scale=wqs[:, c0 : c0 + 256],
+                start=(g == 0),
+                stop=(g == 1),
+            )
+
         out_v = out[0].rearrange("(i w) n -> w i n", w=NW)
+
+        def finish_piece(q):
+            w = NW - 1
+            ob[(w, 4 + q)] = work.tile([P, 256], F32, tag="obq", bufs=4, name="obq%d" % q)
+            cols = slice(256 * q, 256 * q + 256)
+            nc.vector.tensor_tensor(
+                out=ob[(w, 4 + q)][:], in0=py[(w, 4 + q)][:], in1=bias_sb[:, cols], op=mybir.AluOpType.add
+            )
+            nc.sync.dma_start(out=out_v[w][:, cols], in_=ob[(w, 4 + q)][:])
 
         def finish(w, nh):
             ob[(w, nh)] = work.tile([P, 512], F32, tag="ob", bufs=4, name="ob%d_%d" % (w, nh))
@@ -294,5 +323,11 @@ def tile_hieramaskunitattention_pb_kernel(tc, attn, v, proj_w, proj_b, out):
                 oquant(i)
             elif what == "y":
                 stage2(i // 2, i % 2)
+            elif what == "z":
+                piece(i, 0)
+            elif what == "Z":
+                piece(i, 1)
+            elif what == "F":
+                finish_piece(i)
             elif what == "f":
                 finish(i // 2, i % 2)

@@ -26,7 +26,6 @@ NGROUP = 6
 LOADS = "w0 w1 x1 v0 x2 x3 a0 a1 v1 a2 a3 v2 a4 a5 v3 a6 a7 v4 a8 a9 v5 a10 a11"
 PLAN = "w0 w1 w2 c0 w3 q0 w4 w5 w6 W0 W1 w7 W2 W3 a0 A0 c1 a1 A1 q1 b0 b1 a2 s0 A2 c2 a3 s1 o0 A3 q2 O0 a4 s2 A4 c3 a5 s3 y0 o1 A5 q3 O1 a6 s4 y1 A6 c4 a7 s5 y2 o2 A7 f0 q4 O2 a8 s6 y3 A8 f1 c5 a9 s7 y4 o3 A9 q5 O3 a10 s8 y5 A10 a11 s9 y6 o4 B11 f2 O4 s10 y7 f3 s11 o5 O5 z0 Z0 F0 z1 Z1 F1 z2 Z2 F2 z3 Z3 F3"
 ORDER = "BBBBBB"
-ACT_HEADS = 0
 V_LAST = ()
 
 
@@ -76,18 +75,10 @@ def tile_hieramaskunitattention_pb_kernel(tc, attn, v, proj_w, proj_b, out):
         def load_v(s):
             w, g = s // 2, s % 2
             vraw[s] = res.tile([P, 2048], BF16, name="vraw%d" % s)
-            vr = vraw[s][:].rearrange("p (j x f) -> p j x f", x=2, f=256)
-            for x in range(2):
-                h0 = 8 * g + 1 - x
-                heads = v[0, h0 : h0 + 7 : 2, w]
-                if ORDER[s] == "B":
-                    nc.sync.dma_start(out=vr[:, :, x, :], in_=heads.rearrange("h (p j) c -> p h (j c)", j=4))
-                else:
-                    for u in range(2):
-                        nc.sync.dma_start(
-                            out=vr[:, :, x, 128 * u : 128 * u + 128],
-                            in_=heads[:, 256 * u : 256 * u + 256, :].rearrange("h (p e) c -> p h (e c)", e=2),
-                        )
+            nc.sync.dma_start(
+                out=vraw[s][:].rearrange("p (h f) -> p h f", f=256),
+                in_=v[0, 8 * g : 8 * g + 8, w].rearrange("h (p j) c -> p h (j c)", j=4),
+            )
 
         def load_a(c):
             at[c] = res.tile([P, 2, 1024], BF16, name="at%d" % c)
@@ -153,15 +144,10 @@ def tile_hieramaskunitattention_pb_kernel(tc, attn, v, proj_w, proj_b, out):
 
         def vcopy(s):
             vg[s] = work.tile([P, 2048], BF16, tag="vg", align_bytes=64, name="vg%d" % s)
-            nv = 256 * (8 - ACT_HEADS)
-            nc.vector.tensor_copy(
-                out=vg[s][:, 0:nv].rearrange("p (h c i t) -> p h c t i", c=16, i=4, t=4),
-                in_=vraw[s][:, 0:nv].rearrange("p (h t c i) -> p h c t i", t=4, c=16, i=4),
-            )
-            if ACT_HEADS:
-                nc.scalar.copy(
-                    out=vg[s][:, nv:2048].rearrange("p (h c i t) -> p h c t i", c=16, i=4, t=4),
-                    in_=vraw[s][:, nv:2048].rearrange("p (h t c i) -> p h c t i", t=4, c=16, i=4),
+            for x in range(2):
+                nc.vector.tensor_copy(
+                    out=vg[s][:].rearrange("p (j x c i t) -> p x j c t i", x=2, c=16, i=4, t=4)[:, x],
+                    in_=vraw[s][:].rearrange("p (j x t c i) -> p x j c t i", x=2, t=4, c=16, i=4)[:, 1 - x],
                 )
 
         def vquant(s):

@@ -23,7 +23,7 @@ NPAIR = NW * H // 2
 NQUAD = 12
 NGROUP = 6
 
-LOADS = "w0 w1 x1 v0 x2 x3 a0 a1 v1 a2 a3 v2 a4 a5 v3 a6 a7 v4 a8 a9 v5 a10 a11"
+LOADS = "w0 w1 b0 x1 v0 x2 x3 a0 a1 v1 a2 a3 v2 a4 a5 v3 a6 a7 v4 a8 a9 v5 a10 a11"
 PLAN = "w0 w1 w2 c0 w3 q0 w4 w5 w6 W0 W1 w7 W2 W3 a0 A0 c1 a1 A1 q1 b0 b1 a2 s0 A2 c2 a3 s1 o0 A3 q2 O0 a4 s2 A4 c3 a5 s3 y0 o1 A5 q3 O1 a6 s4 y1 A6 c4 a7 s5 y2 o2 A7 f0 q4 O2 a8 s6 y3 A8 f1 c5 a9 s7 y4 o3 A9 q5 O3 a10 s8 y5 A10 a11 s9 y6 o4 B11 f2 O4 s10 y7 f3 s11 o5 O5 z0 Z0 F0 z1 Z1 F1 z2 Z2 F2 z3 Z3 F3"
 ORDER = "BBBBBB"
 V_LAST = ()
@@ -89,10 +89,11 @@ def tile_hieramaskunitattention_pb_kernel(tc, attn, v, proj_w, proj_b, out):
                     in_=attn[0, h0 + hh : h0 + hh + 3 : 2, c // 4].rearrange("h (a r) k -> a h (r k)", r=2),
                 )
 
-        nc.scalar.dma_start(out=brow[0:1, :], in_=proj_b.rearrange("(o n) -> o n", o=1))
         for item in LOADS.split(" "):
             what, i = item[0:1], int(item[1:])
-            if what == "w":
+            if what == "b":
+                nc.sync.dma_start(out=brow[0:1, :], in_=proj_b.rearrange("(o n) -> o n", o=1))
+            elif what == "w":
                 load_w(i, 1)
             elif what == "x":
                 load_w(2 * i, 2)

from contextlib import ExitStack

import concourse.mybir as mybir
from concourse.masks import make_identity

F32 = mybir.dt.float32
BF16 = mybir.dt.bfloat16
U32 = mybir.dt.uint32
U8 = mybir.dt.uint8
I32 = mybir.dt.int32
FP8X4 = mybir.dt.float8_e4m3fn_x4

P = 128
H = 16
NW = 3
KEYS = 512
HD = 64
D = 1024
FLOPS = 2 * H * NW * P * KEYS * HD + 2 * NW * P * D * D

PERIOD = 192
NPAIR = NW * H // 2
NQUAD = 12
NGROUP = 6

LOADS = "w0 w1 b0 x1 v0 x2 x3 a0 a1 v1 a2 a3 v2 a4 a5 v3 a6 a7 v4 a8 a9 v5 a10 a11"
PLAN = "w0 w1 w2 c0 w3 q0 w4 w5 w6 W0 W1 w7 W2 W3 a0 A0 c1 a1 A1 q1 b0 b1 a2 s0 A2 c2 a3 s1 o0 A3 q2 O0 a4 s2 A4 c3 a5 s3 y0 o1 A5 q3 O1 a6 s4 y1 A6 c4 a7 s5 y2 o2 A7 f0 q4 O2 a8 s6 y3 A8 f1 c5 a9 s7 y4 o3 A9 q5 O3 a10 s8 y5 A10 a11 s9 y6 o4 B11 f2 O4 s10 y7 f3 s11 o5 O5 z0 Z0 F0 z1 Z1 F1 z2 Z2 F2 z3 Z3 F3"
ORDER = "BBBBBB"
V_LAST = ()


def tile_hieramaskunitattention_pb_kernel(tc, attn, v, proj_w, proj_b, out):
    nc = tc.nc
    with ExitStack() as ctx:
        const = ctx.enter_context(tc.tile_pool(name="const", bufs=1))
        res = ctx.enter_context(tc.tile_pool(name="res", bufs=1))
        work = ctx.enter_context(tc.tile_pool(name="work", bufs=2))
        psum_t = ctx.enter_context(tc.psum_pool(name="psum_t", bufs=4))
        psum_o = ctx.enter_context(tc.psum_pool(name="psum_o", bufs=2))
        psum_y = ctx.enter_context(tc.psum_pool(name="psum_y", bufs=2))
        ctx.enter_context(tc.manual_schedule())

        ones = const.tile([P, P], BF16)
        nc.vector.memset(ones[:], 1.0)
        ident_b = const.tile([P, P], BF16)
        make_identity(nc, ident_b[:])
        ident_f = const.tile([P, P], F32)
        make_identity(nc, ident_f[:])
        brow = const.tile([P, D], BF16)
        nc.vector.memset(brow[:].bitcast(I32), 0)
        perm = const.tile([P, P], F32)
        nc.vector.tensor_copy(
            out=perm[:].rearrange("p (h a) -> p h a", h=2), in_=ident_f[:].rearrange("p (a h) -> p h a", h=2)
        )
        vq = res.tile([P, (NPAIR + 1) * PERIOD], U32, align_bytes=64)
        vqs = res.tile([P, (NPAIR + 1) * PERIOD], U8, align_bytes=64)
        nc.vector.memset(
            vq[:].bitcast(I32).rearrange("p (a b) -> p a b", b=PERIOD)[:, :, 0:64], 0
        )
        nc.vector.memset(
            vqs[:].bitcast(I32).rearrange("p (a b) -> p a b", b=PERIOD // 4)[:, :, 0:16], 0
        )

        w_sb = {}
        at = {}
        vraw = {}

        def load_w(nt, n):
            t = res.tile([P, n, D], BF16, name="w%d" % nt)
            rows = proj_w[128 * nt : 128 * nt + 128 * n, :]
            nc.sync.dma_start(out=t[:], in_=rows.rearrange("(n p) k -> p n k", p=P))
            for i in range(n):
                w_sb[nt + i] = t[:, i, :]

        def load_v(s):
            w, g = s // 2, s % 2
            vraw[s] = res.tile([P, 2048], BF16, name="vraw%d" % s)
            nc.sync.dma_start(
                out=vraw[s][:].rearrange("p (h f) -> p h f", f=256),
                in_=v[0, 8 * g : 8 * g + 8, w].rearrange("h (p j) c -> p h (j c)", j=4),
            )

        def load_a(c):
            at[c] = res.tile([P, 2, 1024], BF16, name="at%d" % c)
            h0 = 4 * (c % 4)
            for hh in range(2):
                nc.sync.dma_start(
                    out=at[c][hh:P:2, :, :],
                    in_=attn[0, h0 + hh : h0 + hh + 3 : 2, c // 4].rearrange("h (a r) k -> a h (r k)", r=2),
                )

        for item in LOADS.split(" "):
            what, i = item[0:1], int(item[1:])
            if what == "b":
                nc.sync.dma_start(out=brow[0:1, :], in_=proj_b.rearrange("(o n) -> o n", o=1))
            elif what == "w":
                load_w(i, 1)
            elif what == "x":
                load_w(2 * i, 2)
            elif what == "v":
                load_v(i)
            else:
                load_a(i)

        wg = res.tile([P, 2 * 4096], BF16, align_bytes=64)
        wq = res.tile([P, 2 * D], U32, align_bytes=64)
        wqs = res.tile([P, 2 * D], U8, align_bytes=64)

        def wtrans(nt):
            tw = psum_t.tile([P, 8, P], BF16, tag="tp")
            for k in range(8):
                nc.tensor.transpose(tw[:, k, :], w_sb[nt][:, 128 * k : 128 * k + 128], ident_b[:])
            dst = wg[:].rearrange("p (g n t) -> p g n t", g=2, t=4)[:, :, 128 * nt : 128 * nt + 128, :]
            nc.scalar.copy(out=dst, in_=tw[:].rearrange("p (g t) n -> p g n t", g=2))

        def wquant(nh, g):
            if True:
                c0 = D * g + 512 * nh
                nc.vector.quantize_mx(
                    out=wq[:, c0 : c0 + 512].bitcast(FP8X4),
                    scales=wqs[:, c0 : c0 + 512],
                    in_=wg[:, 4 * c0 : 4 * c0 + 2048],
                )

        bias_sb = const.tile([P, D], F32)

        pbs = [psum_y.tile([P, 512], F32, tag="py", name="pb%d" % nh) for nh in range(2)]

        def bias(nh):
            if True:
                pb = pbs[nh]
                nc.tensor.matmul(out=pb[:], lhsT=ones[:], rhs=brow[:, 512 * nh : 512 * nh + 512], start=True, stop=True)
                nc.scalar.copy(out=bias_sb[:, 512 * nh : 512 * nh + 512], in_=pb[:])

        vg = {}
        ag = {}
        aq = {}
        aqs = {}
        po = {}
        og = {}
        oq = {}
        oqs = {}
        py = {}
        ob = {}

        def vcopy(s):
            vg[s] = work.tile([P, 2048], BF16, tag="vg", align_bytes=64, name="vg%d" % s)
            for x in range(2):
                nc.vector.tensor_copy(
                    out=vg[s][:].rearrange("p (j x c i t) -> p x j c t i", x=2, c=16, i=4, t=4)[:, x],
                    in_=vraw[s][:].rearrange("p (j x t c i) -> p x j c t i", x=2, t=4, c=16, i=4)[:, 1 - x],
                )

        def vquant(s):
            for j in range(4):
                c0 = PERIOD * (4 * s + j) + 64
                nc.vector.quantize_mx(
                    out=vq[:, c0 : c0 + 128].bitcast(FP8X4),
                    scales=vqs[:, c0 : c0 + 128],
                    in_=vg[s][:, 512 * j : 512 * j + 512],
                )

        def trans(c, banks):
            if 0 in banks:
                ag[c] = work.tile([P, 2048], BF16, tag="ag", bufs=4, align_bytes=64, name="ag%d" % c)
            dst = ag[c][:].bitcast(F32)
            for b in banks:
                a32 = at[c][:, b, :].bitcast(F32)
                tp = psum_t.tile([P, 4, P], F32, tag="tp")
                for r in range(2):
                    for u in range(2):
                        k0 = 256 * r
                        if ORDER[c // 2] == "B":
                            words = a32[:, k0 + u : k0 + 256 : 2]
                        else:
                            words = a32[:, k0 + 128 * u : k0 + 128 * u + 128]
                        nc.tensor.transpose(tp[:, 2 * r + u, :], words, perm[:])
                o_ap = dst[:, 512 * b : 512 * b + 512].rearrange("p (i s) -> p i s", s=4)
                i_ap = tp[:].rearrange("p s i -> p i s")
                if 2 * c + b in V_LAST:
                    nc.vector.tensor_copy(out=o_ap, in_=i_ap)
                else:
                    nc.scalar.copy(out=o_ap, in_=i_ap)

        def aquant(c, pieces, which):
            if 0 in which:
                aq[c] = work.tile([P, 512], U32, tag="aq", bufs=6, align_bytes=64, name="aq%d" % c)
                aqs[c] = work.tile([P, 512], U8, tag="aqs", bufs=6, align_bytes=64, name="aqs%d" % c)
            n = 512 // pieces
            for i in which:
                nc.vector.quantize_mx(
                    out=aq[c][:, n * i : n * i + n].bitcast(FP8X4),
                    scales=aqs[c][:, n * i : n * i + n],
                    in_=ag[c][:, 4 * n * i : 4 * n * i + 4 * n],
                )

        def stage1(c, pairs):
            s = c // 2
            if c % 2 == 0 and 0 in pairs:
                po[s] = psum_o.tile([P, 4, P], F32, tag="po", name="po%d" % s)
            for jl in pairs:
                j = 2 * (c % 2) + jl
                base = PERIOD * (4 * s + j)
                for hh in range(2):
                    l0 = base + 128 if hh == 0 else base
                    r0 = 256 * jl + 128 * hh
                    nc.tensor.matmul_mx(
                        out=po[s][:, j, :],
                        lhsT=vq[:, l0 : l0 + 128].bitcast(FP8X4),
                        lhsT_scale=vqs[:, l0 : l0 + 128],
                        rhs=aq[c][:, r0 : r0 + 128].bitcast(FP8X4),
                        rhs_scale=aqs[c][:, r0 : r0 + 128],
                        start=(hh == 0),
                        stop=(hh == 1),
                    )

        def ocopy(s):
            og[s] = work.tile([P, 512], BF16, tag="og", align_bytes=64, name="og%d" % s)
            nc.scalar.copy(out=og[s][:].rearrange("p (q t) -> p q t", t=4), in_=po[s][:].rearrange("p t q -> p q t"))

        def oquant(s):
            w, g = s // 2, s % 2
            if g == 0:
                oq[w] = work.tile([P, 256], U32, tag="oq", align_bytes=64, name="oq%d" % w)
                oqs[w] = work.tile([P, 256], U8, tag="oqs", align_bytes=64, name="oqs%d" % w)
            nc.vector.quantize_mx(
                out=oq[w][:, 128 * g : 128 * g + 128].bitcast(FP8X4),
                scales=oqs[w][:, 128 * g : 128 * g + 128],
                in_=og[s][:],
            )

        def stage2(s, nh):
            w, g = s // 2, s % 2
            if g == 0:
                py[(w, nh)] = psum_y.tile([P, 512], F32, tag="py", name="py%d_%d" % (w, nh))
            c0 = D * g + 512 * nh
            nc.tensor.matmul_mx(
                out=py[(w, nh)][:],
                lhsT=oq[w][:, 128 * g : 128 * g + 128].bitcast(FP8X4),
                lhsT_scale=oqs[w][:, 128 * g : 128 * g + 128],
                rhs=wq[:, c0 : c0 + 512].bitcast(FP8X4),
                rhs_scale=wqs[:, c0 : c0 + 512],
                start=(g == 0),
                stop=(g == 1),
            )

        def piece(q, g):
            w = NW - 1
            if g == 0:
                py[(w, 4 + q)] = psum_t.tile([P, 256], F32, tag="tp", name="pz%d" % q)
            c0 = D * g + 256 * q
            nc.tensor.matmul_mx(
                out=py[(w, 4 + q)][:],
                lhsT=oq[w][:, 128 * g : 128 * g + 128].bitcast(FP8X4),
                lhsT_scale=oqs[w][:, 128 * g : 128 * g + 128],
                rhs=wq[:, c0 : c0 + 256].bitcast(FP8X4),
                rhs_scale=wqs[:, c0 : c0 + 256],
                start=(g == 0),
                stop=(g == 1),
            )

        out_v = out[0].rearrange("(i w) n -> w i n", w=NW)

        def finish_piece(q):
            w = NW - 1
            ob[(w, 4 + q)] = work.tile([P, 256], F32, tag="obq", bufs=4, name="obq%d" % q)
            cols = slice(256 * q, 256 * q + 256)
            nc.vector.tensor_tensor(
                out=ob[(w, 4 + q)][:], in0=py[(w, 4 + q)][:], in1=bias_sb[:, cols], op=mybir.AluOpType.add
            )
            nc.sync.dma_start(out=out_v[w][:, cols], in_=ob[(w, 4 + q)][:])

        def finish(w, nh):
            ob[(w, nh)] = work.tile([P, 512], F32, tag="ob", bufs=4, name="ob%d_%d" % (w, nh))
            cols = slice(512 * nh, 512 * nh + 512)
            nc.vector.tensor_tensor(
                out=ob[(w, nh)][:], in0=py[(w, nh)][:], in1=bias_sb[:, cols], op=mybir.AluOpType.add
            )
            nc.sync.dma_start(out=out_v[w][:, cols], in_=ob[(w, nh)][:])

        for item in PLAN.split(" "):
            what, i = item[0:1], int(item[1:]) if len(item) > 1 else 0
            if what == "b":
                bias(i)
            elif what == "w":
                wtrans(i)
            elif what == "W":
                wquant(i // 2, i % 2)
            elif what == "c":
                vcopy(i)
            elif what == "q":
                vquant(i)
            elif what == "a":
                trans(i, (0, 1))
            elif what == "x":
                trans(i // 2, (i % 2,))
            elif what == "H":
                aquant(i // 2, 2, (i % 2,))
            elif what == "S":
                stage1(i // 2, (i % 2,))
            elif what == "A":
                aquant(i, 1, (0,))
            elif what == "B":
                aquant(i, 2, (0, 1))
            elif what == "s":
                stage1(i, (0, 1))
            elif what == "o":
                ocopy(i)
            elif what == "O":
                oquant(i)
            elif what == "y":
                stage2(i // 2, i % 2)
            elif what == "z":
                piece(i, 0)
            elif what == "Z":
                piece(i, 1)
            elif what == "F":
                finish_piece(i)
            elif what == "f":
                finish(i // 2, i % 2)
